import numpy as np
import ml_dtypes


def mxq(x, axis, fmt="e4m3"):
    dtype, down = {"e4m3": (ml_dtypes.float8_e4m3fn, 7), "e5m2": (ml_dtypes.float8_e5m2, 14)}[fmt]
    v = np.moveaxis(np.asarray(x, np.float32).astype(ml_dtypes.bfloat16).astype(np.float64), axis, -1)
    blocks = v.reshape(v.shape[:-1] + (-1, 32))
    amax = np.abs(blocks).max(-1, keepdims=True)
    byte = np.maximum(np.where(amax > 0, np.frexp(amax)[1] - 1 + 127, 0) - down, 1)
    scale = np.exp2(byte - 127.0)
    codes = (blocks / scale).astype(np.float32).astype(dtype).astype(np.float64)
    return np.moveaxis((codes * scale).reshape(v.shape), -1, axis)


WIDE = False


def mx_kscale(k):
    if not WIDE:
        return np.ones(k)
    levels = np.array([10, -10, 5, -5, 0])
    a = np.random.permutation(np.resize(levels, k // 512 * 4)).reshape(k // 512, 4)
    idx = np.arange(k)
    return np.exp2(a[idx // 512, idx % 128 // 32])


BF16 = ml_dtypes.bfloat16


def bf(x):
    return np.asarray(x, np.float32).astype(BF16)


def f64(x):
    return np.asarray(x).astype(np.float64)


B, C, T, P, N, D = 32, 16, 2048, 128, 8, 512
L = T // P
G = L // N


def gelu_tanh(v):
    return 0.5 * v * (1.0 + np.tanh(np.sqrt(2.0 / np.pi) * (v + 0.044715 * v**3)))


def setup_inputs():
    s = mx_kscale(D)
    return {'x': bf(np.random.standard_normal((B, C, T))),
            'emb_W': bf(np.random.standard_normal((P, D)) / np.sqrt(P) * s),
            'emb_b': bf(np.random.standard_normal(D) * 0.2 * s),
            'enc_W1': bf(np.random.standard_normal((N, D, D)) / np.sqrt(D) / s[None, :, None]),
            'enc_b1': bf(np.random.standard_normal((N, D)) * 0.2)}


def reference(x, emb_W, emb_b, enc_W1, enc_b1):
    e = f64(x).reshape(B * C * L, P) @ f64(emb_W) + f64(emb_b)
    e = np.moveaxis(e.reshape(B, C, G, N, D), 3, 0).reshape(N, B * C * G, D)
    a = (mxq(e, 2, 'e4m3') @ mxq(f64(enc_W1), 1, 'e4m3')) + f64(enc_b1)[:, None, :]
    return gelu_tanh(a).reshape(N, B, C, G, D)

@@ -1,0 +1,200 @@
+from contextlib import ExitStack
+
+import concourse.masks as masks
+import concourse.mybir as mybir
+
+BF16 = mybir.dt.bfloat16
+F32 = mybir.dt.float32
+U32 = mybir.dt.uint32
+U8 = mybir.dt.uint8
+FP8X4 = mybir.dt.float8_e4m3fn_x4
+ACT = mybir.ActivationFunctionType
+ADD = mybir.AluOpType.add
+
+P = 128
+PACK = 4
+MODELS = 8
+SAMPLES = 128
+FEATURES = 512
+ROWS = 8
+GROUP_ROWS = 4
+GROUPS = MODELS * ROWS // GROUP_ROWS
+GROUP_COLS = GROUP_ROWS * P
+STORE_ROWS = 2
+
+FLOPS = 2 * MODELS * ROWS * P * FEATURES * (SAMPLES + FEATURES)
+
+
+def tile_model_pa_t_kernel(tc, x, emb_W, emb_b, enc_W1, enc_b1, out):
+    nc = tc.nc
+    x_by_model = x.rearrange("b c t -> (b c t)").rearrange(
+        "(p r n s) -> n p r s", r=ROWS, n=MODELS, s=SAMPLES
+    )
+    out_by_model = out.rearrange("n b c l f -> n (b c l) f").rearrange(
+        "n (p r) f -> n p r f", r=ROWS
+    )
+
+    with ExitStack() as ctx:
+        const = ctx.enter_context(tc.tile_pool(name="const", bufs=1))
+        inputs = ctx.enter_context(tc.tile_pool(name="inputs", bufs=MODELS))
+        work = ctx.enter_context(tc.tile_pool(name="work", bufs=2))
+        results = ctx.enter_context(tc.tile_pool(name="results", bufs=4))
+        psum_x = ctx.enter_context(tc.psum_pool(name="psum_x", bufs=1))
+        psum_e = ctx.enter_context(tc.psum_pool(name="psum_e", bufs=3))
+        psum_o = ctx.enter_context(tc.psum_pool(name="psum_o", bufs=4))
+
+        x_tiles = {}
+        w_tiles = {}
+        b1_tiles = {}
+        xT_tiles = {}
+        w_grouped_tiles = {}
+        w_codes = {}
+        planar_tiles = {}
+        grouped_tiles = {}
+        e_codes = {}
+        o_tiles = {}
+
+        def load_model(n):
+            x_sb = inputs.tile([P, ROWS, SAMPLES], BF16)
+            nc.sync.dma_start(out=x_sb[:], in_=x_by_model[n])
+            x_tiles[n] = x_sb
+            w_sb = inputs.tile([P, PACK, FEATURES], BF16)
+            nc.sync.dma_start(
+                out=w_sb[:], in_=enc_W1[n].rearrange("(p t) f -> p t f", t=PACK)
+            )
+            w_tiles[n] = w_sb
+            b1_sb = inputs.tile([P, FEATURES], BF16)
+            nc.sync.dma_start(out=b1_sb[:], in_=enc_b1[n, :].partition_broadcast(P))
+            b1_tiles[n] = b1_sb
+
+        emb_w_sb = const.tile([P, FEATURES], BF16)
+        emb_b_bf = const.tile([P, PACK], BF16)
+        nc.sync.dma_start(out=emb_w_sb[:], in_=emb_W)
+        nc.sync.dma_start(out=emb_b_bf[:], in_=emb_b.rearrange("(p t) -> p t", t=PACK))
+        for n in range(MODELS):
+            load_model(n)
+
+        identity = const.tile([P, P], BF16)
+        masks.make_identity(nc, identity[:])
+        warm = const.tile([P, 1], F32)
+        nc.vector.memset(warm[:], 0.0)
+        nc.scalar.activation(out=warm[:], in_=warm[:], func=ACT.Gelu_apprx_tanh)
+        emb_w_t = const.tile([P, PACK, P], BF16)
+        nc.vector.tensor_copy(
+            out=emb_w_t[:], in_=emb_w_sb[:].rearrange("s (p t) -> s t p", t=PACK)
+        )
+        emb_b_sb = const.tile([P, PACK], F32)
+        nc.vector.tensor_copy(out=emb_b_sb[:], in_=emb_b_bf[:])
+
+        def transpose_x(n):
+            xT_ps = psum_x.tile([P, ROWS * P], BF16)
+            for r in range(ROWS):
+                nc.tensor.transpose(
+                    xT_ps[:, r * P : (r + 1) * P], x_tiles[n][:, r, :], identity[:]
+                )
+            xT = work.tile([P, ROWS * P], BF16)
+            nc.scalar.copy(out=xT[:], in_=xT_ps[:])
+            xT_tiles[n] = xT
+
+        def regroup(dst, src):
+            nc.vector.tensor_copy(
+                out=dst[:].rearrange("p (c i) t -> p c t i", i=4),
+                in_=src[:].rearrange("p t (c i) -> p c t i", i=4),
+            )
+
+        def quantise(grouped, name):
+            codes = work.tile([P, GROUP_COLS], U32, align_bytes=64, name=name + "_codes")
+            scales = work.tile([P, GROUP_COLS], U8, align_bytes=64, name=name + "_scales")
+            nc.vector.quantize_mx(
+                out=codes[:].bitcast(FP8X4),
+                scales=scales[:],
+                in_=grouped[:].rearrange("p c t -> p (c t)"),
+            )
+            return codes, scales
+
+        def regroup_w(n):
+            w_grouped = work.tile([P, FEATURES, PACK], BF16, align_bytes=64)
+            regroup(w_grouped, w_tiles[n])
+            w_grouped_tiles[n] = w_grouped
+
+        def quantise_w(n):
+            w_codes[n] = quantise(w_grouped_tiles[n], "w")
+
+        def embed(g):
+            n, h = divmod(g, ROWS // GROUP_ROWS)
+            planar = work.tile([P, PACK, GROUP_COLS], BF16)
+            for t in range(PACK):
+                e_ps = psum_e.tile([P, GROUP_COLS], F32)
+                nc.tensor.matmul(
+                    e_ps[:],
+                    lhsT=emb_w_t[:, t, :],
+                    rhs=xT_tiles[n][:, h * GROUP_COLS : (h + 1) * GROUP_COLS],
+                    start=True,
+                    stop=True,
+                )
+                nc.scalar.activation(
+                    out=planar[:, t, :],
+                    in_=e_ps[:],
+                    func=ACT.Identity,
+                    bias=emb_b_sb[:, t : t + 1],
+                )
+            planar_tiles[g] = planar
+
+        def regroup_e(g):
+            grouped = work.tile([P, GROUP_COLS, PACK], BF16, align_bytes=64)
+            regroup(grouped, planar_tiles[g])
+            grouped_tiles[g] = grouped
+
+        def quantise_e(g):
+            e_codes[g] = quantise(grouped_tiles[g], "e")
+
+        def encode(g):
+            n = g // (ROWS // GROUP_ROWS)
+            codes, scales = e_codes[g]
+            wc, ws = w_codes[n]
+            o_sb = results.tile([P, GROUP_ROWS, FEATURES], F32)
+            for m in range(GROUP_ROWS):
+                o_ps = psum_o.tile([P, FEATURES], F32)
+                nc.tensor.matmul_mx(
+                    out=o_ps[:],
+                    lhsT=codes[:, m * P : (m + 1) * P].bitcast(FP8X4),
+                    lhsT_scale=scales[:, m * P : (m + 1) * P],
+                    rhs=wc[:].bitcast(FP8X4),
+                    rhs_scale=ws[:],
+                    start=True,
+                    stop=True,
+                )
+                nc.vector.tensor_tensor(
+                    out=o_sb[:, m, :], in0=o_ps[:], in1=b1_tiles[n][:], op=ADD
+                )
+            o_tiles[g] = o_sb
+
+        def finish(g):
+            n, h = divmod(g, ROWS // GROUP_ROWS)
+            o_sb = o_tiles[g]
+            for m in range(0, GROUP_ROWS, STORE_ROWS):
+                part = o_sb[:, m : m + STORE_ROWS, :]
+                nc.scalar.activation(out=part, in_=part, func=ACT.Gelu_apprx_tanh)
+                r = h * GROUP_ROWS + m
+                nc.sync.dma_start(out=out_by_model[n][:, r : r + STORE_ROWS, :], in_=part)
+
+        transpose_x(0)
+        for step in range(GROUPS + 3):
+            embedding, regrouping, encoding, finishing = step, step - 1, step - 2, step - 3
+            if 0 <= encoding < GROUPS:
+                quantise_e(encoding)
+            if 0 <= regrouping < GROUPS:
+                regroup_e(regrouping)
+            if embedding < GROUPS:
+                if embedding % 2 == 0:
+                    regroup_w(embedding // 2)
+                else:
+                    quantise_w(embedding // 2)
+            if 0 <= finishing < GROUPS:
+                finish(finishing)
+            if 0 <= encoding < GROUPS:
+                encode(encoding)
+            if embedding < GROUPS:
+                embed(embedding)
+                if embedding % 2 == 0 and embedding // 2 + 1 < MODELS:
+                    transpose_x(embedding // 2 + 1)

@@ -54,6 +54,8 @@ def tile_model_pa_t_kernel(tc, x, emb_W, emb_b, enc_W1, enc_b1, out):
         e_codes = {}
         o_tiles = {}
 
+        ctx.enter_context(tc.manual_schedule())
+
         def load_model(n):
             x_sb = inputs.tile([P, ROWS, SAMPLES], BF16)
             nc.sync.dma_start(out=x_sb[:], in_=x_by_model[n])

@@ -45,7 +45,6 @@ def tile_model_pa_t_kernel(tc, x, emb_W, emb_b, enc_W1, enc_b1, out):
 
         x_tiles = {}
         w_tiles = {}
-        b1_tiles = {}
         xT_tiles = {}
         w_grouped_tiles = {}
         w_codes = {}
@@ -53,8 +52,6 @@ def tile_model_pa_t_kernel(tc, x, emb_W, emb_b, enc_W1, enc_b1, out):
         grouped_tiles = {}
         e_codes = {}
         o_tiles = {}
-
-        ctx.enter_context(tc.manual_schedule())
 
         def load_model(n):
             x_sb = inputs.tile([P, ROWS, SAMPLES], BF16)
@@ -65,15 +62,18 @@ def tile_model_pa_t_kernel(tc, x, emb_W, emb_b, enc_W1, enc_b1, out):
                 out=w_sb[:], in_=enc_W1[n].rearrange("(p t) f -> p t f", t=PACK)
             )
             w_tiles[n] = w_sb
-            b1_sb = inputs.tile([P, FEATURES], BF16)
-            nc.sync.dma_start(out=b1_sb[:], in_=enc_b1[n, :].partition_broadcast(P))
-            b1_tiles[n] = b1_sb
 
         emb_w_sb = const.tile([P, FEATURES], BF16)
         emb_b_bf = const.tile([P, PACK], BF16)
         nc.sync.dma_start(out=emb_w_sb[:], in_=emb_W)
         nc.sync.dma_start(out=emb_b_bf[:], in_=emb_b.rearrange("(p t) -> p t", t=PACK))
-        for n in range(MODELS):
+        load_model(0)
+        b1_sb = const.tile([P, MODELS, FEATURES], BF16)
+        nc.sync.dma_start(
+            out=b1_sb[:].rearrange("p n f -> p (n f)"),
+            in_=enc_b1.rearrange("n f -> (n f)").partition_broadcast(P),
+        )
+        for n in range(1, MODELS):
             load_model(n)
 
         identity = const.tile([P, P], BF16)
@@ -167,7 +167,7 @@ def tile_model_pa_t_kernel(tc, x, emb_W, emb_b, enc_W1, enc_b1, out):
                     stop=True,
                 )
                 nc.vector.tensor_tensor(
-                    out=o_sb[:, m, :], in0=o_ps[:], in1=b1_tiles[n][:], op=ADD
+                    out=o_sb[:, m, :], in0=o_ps[:], in1=b1_sb[:, n, :], op=ADD
                 )
             o_tiles[g] = o_sb
 

@@ -10,6 +10,7 @@ U8 = mybir.dt.uint8
 FP8X4 = mybir.dt.float8_e4m3fn_x4
 ACT = mybir.ActivationFunctionType
 ADD = mybir.AluOpType.add
+MULT = mybir.AluOpType.mult
 
 P = 128
 PACK = 4
@@ -21,6 +22,8 @@ GROUP_ROWS = 4
 GROUPS = MODELS * ROWS // GROUP_ROWS
 GROUP_COLS = GROUP_ROWS * P
 STORE_ROWS = 2
+W_PARTS = 2
+W_PART_COLS = FEATURES // W_PARTS
 
 FLOPS = 2 * MODELS * ROWS * P * FEATURES * (SAMPLES + FEATURES)
 
@@ -114,13 +117,34 @@ def tile_model_pa_t_kernel(tc, x, emb_W, emb_b, enc_W1, enc_b1, out):
             )
             return codes, scales
 
-        def regroup_w(n):
-            w_grouped = work.tile([P, FEATURES, PACK], BF16, align_bytes=64)
-            regroup(w_grouped, w_tiles[n])
-            w_grouped_tiles[n] = w_grouped
+        def regroup_w(part):
+            n, h = divmod(part, W_PARTS)
+            w_grouped = work.tile([P, W_PART_COLS, PACK], BF16, align_bytes=64)
+            nc.gpsimd.tensor_scalar(
+                out=w_grouped[:],
+                in0=w_tiles[n][:, :, h * W_PART_COLS : (h + 1) * W_PART_COLS].rearrange(
+                    "p t c -> p c t"
+                ),
+                scalar1=1.0,
+                scalar2=0.0,
+                op0=MULT,
+                op1=ADD,
+            )
+            w_grouped_tiles[part] = w_grouped
 
-        def quantise_w(n):
-            w_codes[n] = quantise(w_grouped_tiles[n], "w")
+        def quantise_w(part):
+            n, h = divmod(part, W_PARTS)
+            if h == 0:
+                w_code_tile = work.tile([P, FEATURES], U32, align_bytes=64, name="w_codes")
+                w_scale_tile = work.tile([P, FEATURES], U8, align_bytes=64, name="w_scales")
+                w_codes[n] = (w_code_tile, w_scale_tile)
+            codes, scales = w_codes[n]
+            cols = slice(h * W_PART_COLS, (h + 1) * W_PART_COLS)
+            nc.vector.quantize_mx(
+                out=codes[:, cols].bitcast(FP8X4),
+                scales=scales[:, cols],
+                in_=w_grouped_tiles[part][:].rearrange("p c t -> p (c t)"),
+            )
 
         def embed(g):
             n, h = divmod(g, ROWS // GROUP_ROWS)
@@ -181,6 +205,8 @@ def tile_model_pa_t_kernel(tc, x, emb_W, emb_b, enc_W1, enc_b1, out):
                 nc.sync.dma_start(out=out_by_model[n][:, r : r + STORE_ROWS, :], in_=part)
 
         transpose_x(0)
+        regroup_w(0)
+        regroup_w(1)
         for step in range(GROUPS + 3):
             embedding, regrouping, encoding, finishing = step, step - 1, step - 2, step - 3
             if 0 <= encoding < GROUPS:
@@ -188,10 +214,9 @@ def tile_model_pa_t_kernel(tc, x, emb_W, emb_b, enc_W1, enc_b1, out):
             if 0 <= regrouping < GROUPS:
                 regroup_e(regrouping)
             if embedding < GROUPS:
-                if embedding % 2 == 0:
-                    regroup_w(embedding // 2)
-                else:
-                    quantise_w(embedding // 2)
+                quantise_w(embedding)
+                if embedding + 2 < GROUPS:
+                    regroup_w(embedding + 2)
             if 0 <= finishing < GROUPS:
                 finish(finishing)
             if 0 <= encoding < GROUPS:

@@ -204,6 +204,7 @@ def tile_model_pa_t_kernel(tc, x, emb_W, emb_b, enc_W1, enc_b1, out):
                 r = h * GROUP_ROWS + m
                 nc.sync.dma_start(out=out_by_model[n][:, r : r + STORE_ROWS, :], in_=part)
 
+        ctx.enter_context(tc.manual_schedule(engines={mybir.EngineType.DVE}))
         transpose_x(0)
         regroup_w(0)
         regroup_w(1)

@@ -21,6 +21,8 @@ ROWS = 8
 GROUP_ROWS = 4
 GROUPS = MODELS * ROWS // GROUP_ROWS
 GROUP_COLS = GROUP_ROWS * P
+DIRECT_COLS = P
+PLANAR_COLS = GROUP_COLS - DIRECT_COLS
 STORE_ROWS = 2
 W_PARTS = 2
 W_PART_COLS = FEATURES // W_PARTS
@@ -103,8 +105,8 @@ def tile_model_pa_t_kernel(tc, x, emb_W, emb_b, enc_W1, enc_b1, out):
 
         def regroup(dst, src):
             nc.vector.tensor_copy(
-                out=dst[:].rearrange("p (c i) t -> p c t i", i=4),
-                in_=src[:].rearrange("p t (c i) -> p c t i", i=4),
+                out=dst.rearrange("p (c i) t -> p c t i", i=4),
+                in_=src.rearrange("p t (c i) -> p c t i", i=4),
             )
 
         def quantise(grouped, name):
@@ -148,13 +150,14 @@ def tile_model_pa_t_kernel(tc, x, emb_W, emb_b, enc_W1, enc_b1, out):
 
         def embed(g):
             n, h = divmod(g, ROWS // GROUP_ROWS)
-            planar = work.tile([P, PACK, GROUP_COLS], BF16)
+            first = h * GROUP_COLS
+            planar = work.tile([P, PACK, PLANAR_COLS], BF16)
             for t in range(PACK):
-                e_ps = psum_e.tile([P, GROUP_COLS], F32)
+                e_ps = psum_e.tile([P, PLANAR_COLS], F32, name="e_ps")
                 nc.tensor.matmul(
                     e_ps[:],
                     lhsT=emb_w_t[:, t, :],
-                    rhs=xT_tiles[n][:, h * GROUP_COLS : (h + 1) * GROUP_COLS],
+                    rhs=xT_tiles[n][:, first + DIRECT_COLS : first + GROUP_COLS],
                     start=True,
                     stop=True,
                 )
@@ -165,11 +168,26 @@ def tile_model_pa_t_kernel(tc, x, emb_W, emb_b, enc_W1, enc_b1, out):
                     bias=emb_b_sb[:, t : t + 1],
                 )
             planar_tiles[g] = planar
+            e_direct = psum_e.tile([P, PACK, DIRECT_COLS], F32, name="e_ps")
+            for t in range(PACK):
+                nc.tensor.matmul(
+                    e_direct[:, t, :],
+                    lhsT=emb_w_t[:, t, :],
+                    rhs=xT_tiles[n][:, first : first + DIRECT_COLS],
+                    start=True,
+                    stop=True,
+                )
+            grouped = work.tile([P, GROUP_COLS, PACK], BF16, align_bytes=64)
+            nc.vector.tensor_tensor(
+                out=grouped[:, 0:DIRECT_COLS, :],
+                in0=e_direct[:].rearrange("p t c -> p c t"),
+                in1=emb_b_sb[:].unsqueeze(1).to_broadcast([P, DIRECT_COLS, PACK]),
+                op=ADD,
+            )
+            grouped_tiles[g] = grouped
 
         def regroup_e(g):
-            grouped = work.tile([P, GROUP_COLS, PACK], BF16, align_bytes=64)
-            regroup(grouped, planar_tiles[g])
-            grouped_tiles[g] = grouped
+            regroup(grouped_tiles[g][:, DIRECT_COLS:GROUP_COLS, :], planar_tiles[g][:])
 
         def quantise_e(g):
             e_codes[g] = quantise(grouped_tiles[g], "e")
@@ -218,11 +236,10 @@ def tile_model_pa_t_kernel(tc, x, emb_W, emb_b, enc_W1, enc_b1, out):
                 quantise_w(embedding)
                 if embedding + 2 < GROUPS:
                     regroup_w(embedding + 2)
+                embed(embedding)
             if 0 <= finishing < GROUPS:
                 finish(finishing)
             if 0 <= encoding < GROUPS:
                 encode(encoding)
-            if embedding < GROUPS:
-                embed(embedding)
-                if embedding % 2 == 0 and embedding // 2 + 1 < MODELS:
-                    transpose_x(embedding // 2 + 1)
+            if embedding < GROUPS and embedding % 2 == 0 and embedding // 2 + 1 < MODELS:
+                transpose_x(embedding // 2 + 1)

@@ -21,8 +21,7 @@ ROWS = 8
 GROUP_ROWS = 4
 GROUPS = MODELS * ROWS // GROUP_ROWS
 GROUP_COLS = GROUP_ROWS * P
-DIRECT_COLS = P
-PLANAR_COLS = GROUP_COLS - DIRECT_COLS
+VECTOR_BLOCKS = 1
 STORE_ROWS = 2
 W_PARTS = 2
 W_PART_COLS = FEATURES // W_PARTS
@@ -53,7 +52,6 @@ def tile_model_pa_t_kernel(tc, x, emb_W, emb_b, enc_W1, enc_b1, out):
         xT_tiles = {}
         w_grouped_tiles = {}
         w_codes = {}
-        planar_tiles = {}
         grouped_tiles = {}
         e_codes = {}
         o_tiles = {}
@@ -70,8 +68,10 @@ def tile_model_pa_t_kernel(tc, x, emb_W, emb_b, enc_W1, enc_b1, out):
 
         emb_w_sb = const.tile([P, FEATURES], BF16)
         emb_b_bf = const.tile([P, PACK], BF16)
+        emb_b_all = const.tile([P, FEATURES], BF16)
         nc.sync.dma_start(out=emb_w_sb[:], in_=emb_W)
         nc.sync.dma_start(out=emb_b_bf[:], in_=emb_b.rearrange("(p t) -> p t", t=PACK))
+        nc.sync.dma_start(out=emb_b_all[:], in_=emb_b.partition_broadcast(P))
         load_model(0)
         b1_sb = const.tile([P, MODELS, FEATURES], BF16)
         nc.sync.dma_start(
@@ -83,6 +83,8 @@ def tile_model_pa_t_kernel(tc, x, emb_W, emb_b, enc_W1, enc_b1, out):
 
         identity = const.tile([P, P], BF16)
         masks.make_identity(nc, identity[:])
+        identity_f32 = const.tile([P, P], F32)
+        masks.make_identity(nc, identity_f32[:])
         warm = const.tile([P, 1], F32)
         nc.vector.memset(warm[:], 0.0)
         nc.scalar.activation(out=warm[:], in_=warm[:], func=ACT.Gelu_apprx_tanh)
@@ -92,6 +94,10 @@ def tile_model_pa_t_kernel(tc, x, emb_W, emb_b, enc_W1, enc_b1, out):
         )
         emb_b_sb = const.tile([P, PACK], F32)
         nc.vector.tensor_copy(out=emb_b_sb[:], in_=emb_b_bf[:])
+        emb_b_rows = const.tile([P, PACK, P], F32)
+        nc.vector.tensor_copy(
+            out=emb_b_rows[:], in_=emb_b_all[:].rearrange("i (p t) -> i t p", t=PACK)
+        )
 
         def transpose_x(n):
             xT_ps = psum_x.tile([P, ROWS * P], BF16)
@@ -102,22 +108,6 @@ def tile_model_pa_t_kernel(tc, x, emb_W, emb_b, enc_W1, enc_b1, out):
             xT = work.tile([P, ROWS * P], BF16)
             nc.scalar.copy(out=xT[:], in_=xT_ps[:])
             xT_tiles[n] = xT
-
-        def regroup(dst, src):
-            nc.vector.tensor_copy(
-                out=dst.rearrange("p (c i) t -> p c t i", i=4),
-                in_=src.rearrange("p t (c i) -> p c t i", i=4),
-            )
-
-        def quantise(grouped, name):
-            codes = work.tile([P, GROUP_COLS], U32, align_bytes=64, name=name + "_codes")
-            scales = work.tile([P, GROUP_COLS], U8, align_bytes=64, name=name + "_scales")
-            nc.vector.quantize_mx(
-                out=codes[:].bitcast(FP8X4),
-                scales=scales[:],
-                in_=grouped[:].rearrange("p c t -> p (c t)"),
-            )
-            return codes, scales
 
         def regroup_w(part):
             n, h = divmod(part, W_PARTS)
@@ -150,47 +140,51 @@ def tile_model_pa_t_kernel(tc, x, emb_W, emb_b, enc_W1, enc_b1, out):
 
         def embed(g):
             n, h = divmod(g, ROWS // GROUP_ROWS)
-            first = h * GROUP_COLS
-            planar = work.tile([P, PACK, PLANAR_COLS], BF16)
-            for t in range(PACK):
-                e_ps = psum_e.tile([P, PLANAR_COLS], F32, name="e_ps")
-                nc.tensor.matmul(
-                    e_ps[:],
-                    lhsT=emb_w_t[:, t, :],
-                    rhs=xT_tiles[n][:, first + DIRECT_COLS : first + GROUP_COLS],
-                    start=True,
-                    stop=True,
-                )
-                nc.scalar.activation(
-                    out=planar[:, t, :],
-                    in_=e_ps[:],
-                    func=ACT.Identity,
-                    bias=emb_b_sb[:, t : t + 1],
-                )
-            planar_tiles[g] = planar
-            e_direct = psum_e.tile([P, PACK, DIRECT_COLS], F32, name="e_ps")
-            for t in range(PACK):
-                nc.tensor.matmul(
-                    e_direct[:, t, :],
-                    lhsT=emb_w_t[:, t, :],
-                    rhs=xT_tiles[n][:, first : first + DIRECT_COLS],
-                    start=True,
-                    stop=True,
-                )
             grouped = work.tile([P, GROUP_COLS, PACK], BF16, align_bytes=64)
-            nc.vector.tensor_tensor(
-                out=grouped[:, 0:DIRECT_COLS, :],
-                in0=e_direct[:].rearrange("p t c -> p c t"),
-                in1=emb_b_sb[:].unsqueeze(1).to_broadcast([P, DIRECT_COLS, PACK]),
-                op=ADD,
-            )
             grouped_tiles[g] = grouped
-
-        def regroup_e(g):
-            regroup(grouped_tiles[g][:, DIRECT_COLS:GROUP_COLS, :], planar_tiles[g][:])
+            for m in range(GROUP_ROWS - 1, -1, -1):
+                by_vector = m < VECTOR_BLOCKS
+                cols = slice(m * P, (m + 1) * P)
+                x_cols = slice(h * GROUP_COLS + m * P, h * GROUP_COLS + (m + 1) * P)
+                e_ps = psum_e.tile([P, PACK, P], F32)
+                for t in range(PACK):
+                    if not by_vector:
+                        nc.tensor.matmul(
+                            e_ps[:, t, :],
+                            lhsT=emb_b_rows[:, t, :],
+                            rhs=identity_f32[:],
+                            is_transpose=True,
+                            start=True,
+                            stop=False,
+                        )
+                    nc.tensor.matmul(
+                        e_ps[:, t, :],
+                        lhsT=emb_w_t[:, t, :],
+                        rhs=xT_tiles[n][:, x_cols],
+                        start=by_vector,
+                        stop=True,
+                    )
+                if by_vector:
+                    nc.vector.tensor_tensor(
+                        out=grouped[:, cols, :],
+                        in0=e_ps[:].rearrange("p t c -> p c t"),
+                        in1=emb_b_sb[:].unsqueeze(1).to_broadcast([P, P, PACK]),
+                        op=ADD,
+                    )
+                else:
+                    nc.scalar.copy(
+                        out=grouped[:, cols, :], in_=e_ps[:].rearrange("p t c -> p c t")
+                    )
 
         def quantise_e(g):
-            e_codes[g] = quantise(grouped_tiles[g], "e")
+            codes = work.tile([P, GROUP_COLS], U32, align_bytes=64, name="e_codes")
+            scales = work.tile([P, GROUP_COLS], U8, align_bytes=64, name="e_scales")
+            nc.vector.quantize_mx(
+                out=codes[:].bitcast(FP8X4),
+                scales=scales[:],
+                in_=grouped_tiles[g][:].rearrange("p c t -> p (c t)"),
+            )
+            e_codes[g] = (codes, scales)
 
         def encode(g):
             n = g // (ROWS // GROUP_ROWS)
@@ -226,16 +220,17 @@ def tile_model_pa_t_kernel(tc, x, emb_W, emb_b, enc_W1, enc_b1, out):
         transpose_x(0)
         regroup_w(0)
         regroup_w(1)
-        for step in range(GROUPS + 3):
-            embedding, regrouping, encoding, finishing = step, step - 1, step - 2, step - 3
+        quantise_w(0)
+        regroup_w(2)
+        for step in range(GROUPS + 2):
+            embedding, encoding, finishing = step, step - 1, step - 2
             if 0 <= encoding < GROUPS:
                 quantise_e(encoding)
-            if 0 <= regrouping < GROUPS:
-                regroup_e(regrouping)
+            if embedding + 1 < GROUPS:
+                quantise_w(embedding + 1)
+                if embedding + 3 < GROUPS:
+                    regroup_w(embedding + 3)
             if embedding < GROUPS:
-                quantise_w(embedding)
-                if embedding + 2 < GROUPS:
-                    regroup_w(embedding + 2)
                 embed(embedding)
             if 0 <= finishing < GROUPS:
                 finish(finishing)

@@ -42,6 +42,7 @@ def tile_model_pa_t_kernel(tc, x, emb_W, emb_b, enc_W1, enc_b1, out):
         const = ctx.enter_context(tc.tile_pool(name="const", bufs=1))
         inputs = ctx.enter_context(tc.tile_pool(name="inputs", bufs=MODELS))
         work = ctx.enter_context(tc.tile_pool(name="work", bufs=2))
+        turned = ctx.enter_context(tc.tile_pool(name="turned", bufs=4))
         results = ctx.enter_context(tc.tile_pool(name="results", bufs=4))
         psum_x = ctx.enter_context(tc.psum_pool(name="psum_x", bufs=1))
         psum_e = ctx.enter_context(tc.psum_pool(name="psum_e", bufs=3))
@@ -53,6 +54,7 @@ def tile_model_pa_t_kernel(tc, x, emb_W, emb_b, enc_W1, enc_b1, out):
         w_grouped_tiles = {}
         w_codes = {}
         grouped_tiles = {}
+        e_banks = {}
         e_codes = {}
         o_tiles = {}
 
@@ -99,29 +101,40 @@ def tile_model_pa_t_kernel(tc, x, emb_W, emb_b, enc_W1, enc_b1, out):
             out=emb_b_rows[:], in_=emb_b_all[:].rearrange("i (p t) -> i t p", t=PACK)
         )
 
-        def transpose_x(n):
-            xT_ps = psum_x.tile([P, ROWS * P], BF16)
-            for r in range(ROWS):
+        def transpose_x(g):
+            n, h = divmod(g, ROWS // GROUP_ROWS)
+            xT_ps = psum_x.tile([P, GROUP_COLS], BF16)
+            for m in range(GROUP_ROWS):
                 nc.tensor.transpose(
-                    xT_ps[:, r * P : (r + 1) * P], x_tiles[n][:, r, :], identity[:]
+                    xT_ps[:, m * P : (m + 1) * P],
+                    x_tiles[n][:, h * GROUP_ROWS + m, :],
+                    identity[:],
                 )
-            xT = work.tile([P, ROWS * P], BF16)
-            nc.scalar.copy(out=xT[:], in_=xT_ps[:])
-            xT_tiles[n] = xT
+            xT_tiles[g] = xT_ps
+
+        def copy_xT(g):
+            xT = turned.tile([P, GROUP_COLS], BF16)
+            nc.scalar.copy(out=xT[:], in_=xT_tiles[g][:])
+            xT_tiles[g] = xT
 
         def regroup_w(part):
             n, h = divmod(part, W_PARTS)
             w_grouped = work.tile([P, W_PART_COLS, PACK], BF16, align_bytes=64)
-            nc.gpsimd.tensor_scalar(
-                out=w_grouped[:],
-                in0=w_tiles[n][:, :, h * W_PART_COLS : (h + 1) * W_PART_COLS].rearrange(
-                    "p t c -> p c t"
-                ),
-                scalar1=1.0,
-                scalar2=0.0,
-                op0=MULT,
-                op1=ADD,
-            )
+            w_part = w_tiles[n][:, :, h * W_PART_COLS : (h + 1) * W_PART_COLS]
+            if n == 0:
+                nc.vector.tensor_copy(
+                    out=w_grouped[:].rearrange("p (c i) t -> p c t i", i=4),
+                    in_=w_part.rearrange("p t (c i) -> p c t i", i=4),
+                )
+            else:
+                nc.gpsimd.tensor_scalar(
+                    out=w_grouped[:],
+                    in0=w_part.rearrange("p t c -> p c t"),
+                    scalar1=1.0,
+                    scalar2=0.0,
+                    op0=MULT,
+                    op1=ADD,
+                )
             w_grouped_tiles[part] = w_grouped
 
         def quantise_w(part):
@@ -138,43 +151,44 @@ def tile_model_pa_t_kernel(tc, x, emb_W, emb_b, enc_W1, enc_b1, out):
                 in_=w_grouped_tiles[part][:].rearrange("p c t -> p (c t)"),
             )
 
-        def embed(g):
-            n, h = divmod(g, ROWS // GROUP_ROWS)
-            grouped = work.tile([P, GROUP_COLS, PACK], BF16, align_bytes=64)
-            grouped_tiles[g] = grouped
-            for m in range(GROUP_ROWS - 1, -1, -1):
-                by_vector = m < VECTOR_BLOCKS
-                cols = slice(m * P, (m + 1) * P)
-                x_cols = slice(h * GROUP_COLS + m * P, h * GROUP_COLS + (m + 1) * P)
-                e_ps = psum_e.tile([P, PACK, P], F32)
+        def embed_block(g, m):
+            by_vector = m < VECTOR_BLOCKS
+            e_ps = psum_e.tile([P, PACK, P], F32)
+            if not by_vector:
                 for t in range(PACK):
-                    if not by_vector:
-                        nc.tensor.matmul(
-                            e_ps[:, t, :],
-                            lhsT=emb_b_rows[:, t, :],
-                            rhs=identity_f32[:],
-                            is_transpose=True,
-                            start=True,
-                            stop=False,
-                        )
                     nc.tensor.matmul(
                         e_ps[:, t, :],
-                        lhsT=emb_w_t[:, t, :],
-                        rhs=xT_tiles[n][:, x_cols],
-                        start=by_vector,
-                        stop=True,
+                        lhsT=emb_b_rows[:, t, :],
+                        rhs=identity_f32[:],
+                        is_transpose=True,
+                        start=(t == 0),
+                        stop=False,
                     )
-                if by_vector:
-                    nc.vector.tensor_tensor(
-                        out=grouped[:, cols, :],
-                        in0=e_ps[:].rearrange("p t c -> p c t"),
-                        in1=emb_b_sb[:].unsqueeze(1).to_broadcast([P, P, PACK]),
-                        op=ADD,
-                    )
-                else:
-                    nc.scalar.copy(
-                        out=grouped[:, cols, :], in_=e_ps[:].rearrange("p t c -> p c t")
-                    )
+            for t in range(PACK):
+                nc.tensor.matmul(
+                    e_ps[:, t, :],
+                    lhsT=emb_w_t[:, t, :],
+                    rhs=xT_tiles[g][:, m * P : (m + 1) * P],
+                    start=(by_vector and t == 0),
+                    stop=(t == PACK - 1),
+                )
+            e_banks[(g, m)] = e_ps
+
+        def empty_block(g, m):
+            if m == GROUP_ROWS - 1:
+                grouped = work.tile([P, GROUP_COLS, PACK], BF16, align_bytes=64)
+                grouped_tiles[g] = grouped
+            dst = grouped_tiles[g][:, m * P : (m + 1) * P, :]
+            src = e_banks[(g, m)][:].rearrange("p t c -> p c t")
+            if m < VECTOR_BLOCKS:
+                nc.vector.tensor_tensor(
+                    out=dst,
+                    in0=src,
+                    in1=emb_b_sb[:].unsqueeze(1).to_broadcast([P, P, PACK]),
+                    op=ADD,
+                )
+            else:
+                nc.scalar.copy(out=dst, in_=src)
 
         def quantise_e(g):
             codes = work.tile([P, GROUP_COLS], U32, align_bytes=64, name="e_codes")
@@ -190,9 +204,10 @@ def tile_model_pa_t_kernel(tc, x, emb_W, emb_b, enc_W1, enc_b1, out):
             n = g // (ROWS // GROUP_ROWS)
             codes, scales = e_codes[g]
             wc, ws = w_codes[n]
-            o_sb = results.tile([P, GROUP_ROWS, FEATURES], F32)
+            banks = []
             for m in range(GROUP_ROWS):
                 o_ps = psum_o.tile([P, FEATURES], F32)
+                banks.append(o_ps)
                 nc.tensor.matmul_mx(
                     out=o_ps[:],
                     lhsT=codes[:, m * P : (m + 1) * P].bitcast(FP8X4),
@@ -202,8 +217,14 @@ def tile_model_pa_t_kernel(tc, x, emb_W, emb_b, enc_W1, enc_b1, out):
                     start=True,
                     stop=True,
                 )
+            o_tiles[g] = banks
+
+        def add_bias(g):
+            n = g // (ROWS // GROUP_ROWS)
+            o_sb = results.tile([P, GROUP_ROWS, FEATURES], F32)
+            for m in range(GROUP_ROWS):
                 nc.vector.tensor_tensor(
-                    out=o_sb[:, m, :], in0=o_ps[:], in1=b1_sb[:, n, :], op=ADD
+                    out=o_sb[:, m, :], in0=o_tiles[g][m][:], in1=b1_sb[:, n, :], op=ADD
                 )
             o_tiles[g] = o_sb
 
@@ -216,25 +237,46 @@ def tile_model_pa_t_kernel(tc, x, emb_W, emb_b, enc_W1, enc_b1, out):
                 r = h * GROUP_ROWS + m
                 nc.sync.dma_start(out=out_by_model[n][:, r : r + STORE_ROWS, :], in_=part)
 
-        ctx.enter_context(tc.manual_schedule(engines={mybir.EngineType.DVE}))
+        scalar_blocks = list(range(GROUP_ROWS - 1, VECTOR_BLOCKS - 1, -1))
+        vector_blocks = list(range(VECTOR_BLOCKS - 1, -1, -1))
+        ctx.enter_context(tc.manual_schedule())
         transpose_x(0)
+        copy_xT(0)
+        transpose_x(1)
+        copy_xT(1)
         regroup_w(0)
         regroup_w(1)
         quantise_w(0)
         regroup_w(2)
+        quantise_w(1)
+        regroup_w(3)
+        for m in scalar_blocks:
+            embed_block(0, m)
         for step in range(GROUPS + 2):
             embedding, encoding, finishing = step, step - 1, step - 2
             if 0 <= encoding < GROUPS:
                 quantise_e(encoding)
-            if embedding + 1 < GROUPS:
+            if 1 <= embedding < GROUPS - 1:
                 quantise_w(embedding + 1)
                 if embedding + 3 < GROUPS:
                     regroup_w(embedding + 3)
             if embedding < GROUPS:
-                embed(embedding)
-            if 0 <= finishing < GROUPS:
-                finish(finishing)
+                for m in scalar_blocks:
+                    empty_block(embedding, m)
+                for m in vector_blocks:
+                    embed_block(embedding, m)
             if 0 <= encoding < GROUPS:
                 encode(encoding)
-            if embedding < GROUPS and embedding % 2 == 0 and embedding // 2 + 1 < MODELS:
-                transpose_x(embedding // 2 + 1)
+            if embedding < GROUPS:
+                for m in vector_blocks:
+                    empty_block(embedding, m)
+            if 0 <= encoding < GROUPS:
+                add_bias(encoding)
+            if 0 <= finishing < GROUPS:
+                finish(finishing)
+            if embedding + 2 < GROUPS:
+                transpose_x(embedding + 2)
+                copy_xT(embedding + 2)
+            if embedding + 1 < GROUPS:
+                for m in scalar_blocks:
+                    embed_block(embedding + 1, m)

@@ -21,7 +21,10 @@ ROWS = 8
 GROUP_ROWS = 4
 GROUPS = MODELS * ROWS // GROUP_ROWS
 GROUP_COLS = GROUP_ROWS * P
-VECTOR_BLOCKS = 1
+LONG_RUNS = True
+EARLY_LAST = True
+FINE_END = True
+TWO_EVERY = 4
 STORE_ROWS = 2
 W_PARTS = 2
 W_PART_COLS = FEATURES // W_PARTS
@@ -58,10 +61,16 @@ def tile_model_pa_t_kernel(tc, x, emb_W, emb_b, enc_W1, enc_b1, out):
         e_codes = {}
         o_tiles = {}
 
-        def load_model(n):
-            x_sb = inputs.tile([P, ROWS, SAMPLES], BF16)
-            nc.sync.dma_start(out=x_sb[:], in_=x_by_model[n])
-            x_tiles[n] = x_sb
+        def vector_blocks_of(g):
+            return 2 if TWO_EVERY and g % TWO_EVERY == 0 else 1
+
+        def load_x(n, first, last):
+            if first == 0:
+                x_sb = inputs.tile([P, ROWS, SAMPLES], BF16, name="x_sb")
+                x_tiles[n] = x_sb
+            nc.sync.dma_start(out=x_tiles[n][:, first:last, :], in_=x_by_model[n][:, first:last, :])
+
+        def load_w(n):
             w_sb = inputs.tile([P, PACK, FEATURES], BF16)
             nc.sync.dma_start(
                 out=w_sb[:], in_=enc_W1[n].rearrange("(p t) f -> p t f", t=PACK)
@@ -71,17 +80,22 @@ def tile_model_pa_t_kernel(tc, x, emb_W, emb_b, enc_W1, enc_b1, out):
         emb_w_sb = const.tile([P, FEATURES], BF16)
         emb_b_bf = const.tile([P, PACK], BF16)
         emb_b_all = const.tile([P, FEATURES], BF16)
+        load_x(0, 0, GROUP_ROWS)
         nc.sync.dma_start(out=emb_w_sb[:], in_=emb_W)
         nc.sync.dma_start(out=emb_b_bf[:], in_=emb_b.rearrange("(p t) -> p t", t=PACK))
         nc.sync.dma_start(out=emb_b_all[:], in_=emb_b.partition_broadcast(P))
-        load_model(0)
+        load_x(0, GROUP_ROWS, ROWS)
+        load_w(0)
+        load_x(1, 0, ROWS)
         b1_sb = const.tile([P, MODELS, FEATURES], BF16)
         nc.sync.dma_start(
             out=b1_sb[:].rearrange("p n f -> p (n f)"),
             in_=enc_b1.rearrange("n f -> (n f)").partition_broadcast(P),
         )
         for n in range(1, MODELS):
-            load_model(n)
+            load_w(n)
+            if n + 1 < MODELS:
+                load_x(n + 1, 0, ROWS)
 
         identity = const.tile([P, P], BF16)
         masks.make_identity(nc, identity[:])
@@ -151,10 +165,10 @@ def tile_model_pa_t_kernel(tc, x, emb_W, emb_b, enc_W1, enc_b1, out):
                 in_=w_grouped_tiles[part][:].rearrange("p c t -> p (c t)"),
             )
 
-        def embed_block(g, m):
-            by_vector = m < VECTOR_BLOCKS
+        def lay_bias(g, m):
             e_ps = psum_e.tile([P, PACK, P], F32)
-            if not by_vector:
+            e_banks[(g, m)] = e_ps
+            if m >= vector_blocks_of(g):
                 for t in range(PACK):
                     nc.tensor.matmul(
                         e_ps[:, t, :],
@@ -164,15 +178,27 @@ def tile_model_pa_t_kernel(tc, x, emb_W, emb_b, enc_W1, enc_b1, out):
                         start=(t == 0),
                         stop=False,
                     )
+
+        def multiply_block(g, m):
             for t in range(PACK):
                 nc.tensor.matmul(
-                    e_ps[:, t, :],
+                    e_banks[(g, m)][:, t, :],
                     lhsT=emb_w_t[:, t, :],
                     rhs=xT_tiles[g][:, m * P : (m + 1) * P],
-                    start=(by_vector and t == 0),
+                    start=(m < vector_blocks_of(g) and t == 0),
                     stop=(t == PACK - 1),
                 )
-            e_banks[(g, m)] = e_ps
+
+        def embed_blocks(g, blocks):
+            if LONG_RUNS:
+                for m in blocks:
+                    lay_bias(g, m)
+                for m in blocks:
+                    multiply_block(g, m)
+            else:
+                for m in blocks:
+                    lay_bias(g, m)
+                    multiply_block(g, m)
 
         def empty_block(g, m):
             if m == GROUP_ROWS - 1:
@@ -180,7 +206,7 @@ def tile_model_pa_t_kernel(tc, x, emb_W, emb_b, enc_W1, enc_b1, out):
                 grouped_tiles[g] = grouped
             dst = grouped_tiles[g][:, m * P : (m + 1) * P, :]
             src = e_banks[(g, m)][:].rearrange("p t c -> p c t")
-            if m < VECTOR_BLOCKS:
+            if m < vector_blocks_of(g):
                 nc.vector.tensor_tensor(
                     out=dst,
                     in0=src,
@@ -231,14 +257,15 @@ def tile_model_pa_t_kernel(tc, x, emb_W, emb_b, enc_W1, enc_b1, out):
         def finish(g):
             n, h = divmod(g, ROWS // GROUP_ROWS)
             o_sb = o_tiles[g]
-            for m in range(0, GROUP_ROWS, STORE_ROWS):
-                part = o_sb[:, m : m + STORE_ROWS, :]
+            rows = 1 if FINE_END and g == GROUPS - 1 else STORE_ROWS
+            for m in range(0, GROUP_ROWS, rows):
+                part = o_sb[:, m : m + rows, :]
                 nc.scalar.activation(out=part, in_=part, func=ACT.Gelu_apprx_tanh)
                 r = h * GROUP_ROWS + m
-                nc.sync.dma_start(out=out_by_model[n][:, r : r + STORE_ROWS, :], in_=part)
+                nc.sync.dma_start(out=out_by_model[n][:, r : r + rows, :], in_=part)
 
-        scalar_blocks = list(range(GROUP_ROWS - 1, VECTOR_BLOCKS - 1, -1))
-        vector_blocks = list(range(VECTOR_BLOCKS - 1, -1, -1))
+        ahead = [3, 2, 1]
+        last = GROUPS - 1
         ctx.enter_context(tc.manual_schedule())
         transpose_x(0)
         copy_xT(0)
@@ -250,26 +277,25 @@ def tile_model_pa_t_kernel(tc, x, emb_W, emb_b, enc_W1, enc_b1, out):
         regroup_w(2)
         quantise_w(1)
         regroup_w(3)
-        for m in scalar_blocks:
-            embed_block(0, m)
+        embed_blocks(0, ahead)
         for step in range(GROUPS + 2):
             embedding, encoding, finishing = step, step - 1, step - 2
-            if 0 <= encoding < GROUPS:
+            if 0 <= encoding < GROUPS and not (EARLY_LAST and encoding == last):
                 quantise_e(encoding)
             if 1 <= embedding < GROUPS - 1:
                 quantise_w(embedding + 1)
                 if embedding + 3 < GROUPS:
                     regroup_w(embedding + 3)
             if embedding < GROUPS:
-                for m in scalar_blocks:
+                for m in ahead:
                     empty_block(embedding, m)
-                for m in vector_blocks:
-                    embed_block(embedding, m)
+                embed_blocks(embedding, [0])
             if 0 <= encoding < GROUPS:
                 encode(encoding)
             if embedding < GROUPS:
-                for m in vector_blocks:
-                    empty_block(embedding, m)
+                empty_block(embedding, 0)
+            if EARLY_LAST and embedding == last:
+                quantise_e(embedding)
             if 0 <= encoding < GROUPS:
                 add_bias(encoding)
             if 0 <= finishing < GROUPS:
@@ -278,5 +304,4 @@ def tile_model_pa_t_kernel(tc, x, emb_W, emb_b, enc_W1, enc_b1, out):
                 transpose_x(embedding + 2)
                 copy_xT(embedding + 2)
             if embedding + 1 < GROUPS:
-                for m in scalar_blocks:
-                    embed_block(embedding + 1, m)
+                embed_blocks(embedding + 1, ahead)

@@ -21,7 +21,7 @@ ROWS = 8
 GROUP_ROWS = 4
 GROUPS = MODELS * ROWS // GROUP_ROWS
 GROUP_COLS = GROUP_ROWS * P
-LONG_RUNS = True
+LONG_RUNS = False
 EARLY_LAST = True
 FINE_END = True
 TWO_EVERY = 4

@@ -88,12 +88,19 @@ def tile_model_pa_t_kernel(tc, x, emb_W, emb_b, enc_W1, enc_b1, out):
         load_w(0)
         load_x(1, 0, ROWS)
         b1_sb = const.tile([P, MODELS, FEATURES], BF16)
-        nc.sync.dma_start(
-            out=b1_sb[:].rearrange("p n f -> p (n f)"),
-            in_=enc_b1.rearrange("n f -> (n f)").partition_broadcast(P),
-        )
+
+        def load_b1(first, last):
+            nc.sync.dma_start(
+                out=b1_sb[:, first:last, :].rearrange("p n f -> p (n f)"),
+                in_=enc_b1[first:last, :].rearrange("n f -> (n f)").partition_broadcast(P),
+            )
+
         for n in range(1, MODELS):
             load_w(n)
+            if n == 1:
+                load_b1(0, 2)
+            if n == 2:
+                load_b1(2, MODELS)
             if n + 1 < MODELS:
                 load_x(n + 1, 0, ROWS)
 
@@ -135,7 +142,7 @@ def tile_model_pa_t_kernel(tc, x, emb_W, emb_b, enc_W1, enc_b1, out):
             n, h = divmod(part, W_PARTS)
             w_grouped = work.tile([P, W_PART_COLS, PACK], BF16, align_bytes=64)
             w_part = w_tiles[n][:, :, h * W_PART_COLS : (h + 1) * W_PART_COLS]
-            if n == 0:
+            if n < 2:
                 nc.vector.tensor_copy(
                     out=w_grouped[:].rearrange("p (c i) t -> p c t i", i=4),
                     in_=w_part.rearrange("p t (c i) -> p c t i", i=4),
@@ -274,14 +281,15 @@ def tile_model_pa_t_kernel(tc, x, emb_W, emb_b, enc_W1, enc_b1, out):
         regroup_w(0)
         regroup_w(1)
         quantise_w(0)
-        regroup_w(2)
         quantise_w(1)
-        regroup_w(3)
         embed_blocks(0, ahead)
         for step in range(GROUPS + 2):
             embedding, encoding, finishing = step, step - 1, step - 2
             if 0 <= encoding < GROUPS and not (EARLY_LAST and encoding == last):
                 quantise_e(encoding)
+            if embedding == 1:
+                regroup_w(2)
+                regroup_w(3)
             if 1 <= embedding < GROUPS - 1:
                 quantise_w(embedding + 1)
                 if embedding + 3 < GROUPS:

@@ -79,11 +79,12 @@ def tile_model_pa_t_kernel(tc, x, emb_W, emb_b, enc_W1, enc_b1, out):
 
         emb_w_sb = const.tile([P, FEATURES], BF16)
         emb_b_bf = const.tile([P, PACK], BF16)
-        emb_b_all = const.tile([P, FEATURES], BF16)
+        b1_first = const.tile([P, FEATURES], BF16)
+        nc.vector.memset(b1_first[:], 0.0)
         load_x(0, 0, GROUP_ROWS)
         nc.sync.dma_start(out=emb_w_sb[:], in_=emb_W)
         nc.sync.dma_start(out=emb_b_bf[:], in_=emb_b.rearrange("(p t) -> p t", t=PACK))
-        nc.sync.dma_start(out=emb_b_all[:], in_=emb_b.partition_broadcast(P))
+        nc.sync.dma_start(out=b1_first[0:1, :], in_=enc_b1[0:1, :])
         load_x(0, GROUP_ROWS, ROWS)
         load_w(0)
         load_x(1, 0, ROWS)
@@ -97,10 +98,8 @@ def tile_model_pa_t_kernel(tc, x, emb_W, emb_b, enc_W1, enc_b1, out):
 
         for n in range(1, MODELS):
             load_w(n)
-            if n == 1:
-                load_b1(0, 2)
             if n == 2:
-                load_b1(2, MODELS)
+                load_b1(1, MODELS)
             if n + 1 < MODELS:
                 load_x(n + 1, 0, ROWS)
 
@@ -118,9 +117,27 @@ def tile_model_pa_t_kernel(tc, x, emb_W, emb_b, enc_W1, enc_b1, out):
         emb_b_sb = const.tile([P, PACK], F32)
         nc.vector.tensor_copy(out=emb_b_sb[:], in_=emb_b_bf[:])
         emb_b_rows = const.tile([P, PACK, P], F32)
-        nc.vector.tensor_copy(
-            out=emb_b_rows[:], in_=emb_b_all[:].rearrange("i (p t) -> i t p", t=PACK)
-        )
+
+        def spread_first_biases():
+            rows_ps = psum_o.tile([P, PACK, P], F32, name="o_ps")
+            for t in range(PACK):
+                nc.tensor.matmul(
+                    rows_ps[:, t, :],
+                    lhsT=emb_b_bf[:, t : t + 1].to_broadcast([P, P]),
+                    rhs=identity[:],
+                    start=(t == 0),
+                    stop=(t == PACK - 1),
+                )
+            nc.vector.tensor_copy(out=emb_b_rows[:], in_=rows_ps[:])
+            b1_ps = psum_o.tile([P, FEATURES], F32, name="o_ps")
+            nc.tensor.matmul(
+                b1_ps[:],
+                lhsT=identity[:, 0:1].to_broadcast([P, P]),
+                rhs=b1_first[:],
+                start=True,
+                stop=True,
+            )
+            nc.vector.tensor_copy(out=b1_sb[:, 0, :], in_=b1_ps[:])
 
         def transpose_x(g):
             n, h = divmod(g, ROWS // GROUP_ROWS)
@@ -276,6 +293,7 @@ def tile_model_pa_t_kernel(tc, x, emb_W, emb_b, enc_W1, enc_b1, out):
         ctx.enter_context(tc.manual_schedule())
         transpose_x(0)
         copy_xT(0)
+        spread_first_biases()
         transpose_x(1)
         copy_xT(1)
         regroup_w(0)

@@ -19,15 +19,14 @@ SAMPLES = 128
 FEATURES = 512
 ROWS = 8
 GROUP_ROWS = 4
-GROUPS = MODELS * ROWS // GROUP_ROWS
+HALVES = ROWS // GROUP_ROWS
+GROUPS = MODELS * HALVES
 GROUP_COLS = GROUP_ROWS * P
-LONG_RUNS = False
-EARLY_LAST = True
-FINE_END = True
-TWO_EVERY = 4
-STORE_ROWS = 2
+STORE_ROWS = 4
 W_PARTS = 2
 W_PART_COLS = FEATURES // W_PARTS
+PLAIN_GROUPS = 4
+VECTOR_MODELS = 1
 
 FLOPS = 2 * MODELS * ROWS * P * FEATURES * (SAMPLES + FEATURES)
 
@@ -59,10 +58,12 @@ def tile_model_pa_t_kernel(tc, x, emb_W, emb_b, enc_W1, enc_b1, out):
         grouped_tiles = {}
         e_banks = {}
         e_codes = {}
+        o_banks = {}
         o_tiles = {}
+        b1_banks = []
 
         def vector_blocks_of(g):
-            return 2 if TWO_EVERY and g % TWO_EVERY == 0 else 1
+            return 1 if g < 3 else 2 if g % 3 == 0 else 1
 
         def load_x(n, first, last):
             if first == 0:
@@ -79,27 +80,36 @@ def tile_model_pa_t_kernel(tc, x, emb_W, emb_b, enc_W1, enc_b1, out):
 
         emb_w_sb = const.tile([P, FEATURES], BF16)
         emb_b_bf = const.tile([P, PACK], BF16)
-        b1_first = const.tile([P, FEATURES], BF16)
-        nc.vector.memset(b1_first[:], 0.0)
+        emb_b_row = const.tile([P, FEATURES], BF16)
+        b1_row = const.tile([P, FEATURES], BF16)
+        first_row = const.tile([P, P], BF16)
+        nc.vector.memset(emb_b_row[:], 0.0)
+        nc.vector.memset(first_row[:], 0.0)
+        nc.vector.memset(first_row[0:1, :], 1.0)
+        nc.vector.memset(b1_row[:], 0.0)
         load_x(0, 0, GROUP_ROWS)
         nc.sync.dma_start(out=emb_w_sb[:], in_=emb_W)
-        nc.sync.dma_start(out=emb_b_bf[:], in_=emb_b.rearrange("(p t) -> p t", t=PACK))
-        nc.sync.dma_start(out=b1_first[0:1, :], in_=enc_b1[0:1, :])
-        load_x(0, GROUP_ROWS, ROWS)
+        nc.sync.dma_start(out=emb_b_row[0:1, :], in_=emb_b.rearrange("(o f) -> o f", o=1))
         load_w(0)
+        nc.sync.dma_start(out=emb_b_bf[:], in_=emb_b.rearrange("(p t) -> p t", t=PACK))
+        load_x(0, GROUP_ROWS, ROWS)
+        nc.sync.dma_start(out=b1_row[0:1, :], in_=enc_b1[0:1, :])
         load_x(1, 0, ROWS)
         b1_sb = const.tile([P, MODELS, FEATURES], BF16)
+        emb_b_all = const.tile([P, FEATURES], BF16)
 
-        def load_b1(first, last):
+        def load_spread():
             nc.sync.dma_start(
-                out=b1_sb[:, first:last, :].rearrange("p n f -> p (n f)"),
-                in_=enc_b1[first:last, :].rearrange("n f -> (n f)").partition_broadcast(P),
+                out=b1_sb[:, 1:MODELS, :].rearrange("p n f -> p (n f)"),
+                in_=enc_b1[1:MODELS, :].rearrange("n f -> (n f)").partition_broadcast(P),
             )
 
         for n in range(1, MODELS):
             load_w(n)
+            if n == 1:
+                nc.sync.dma_start(out=emb_b_all[:], in_=emb_b.partition_broadcast(P))
             if n == 2:
-                load_b1(1, MODELS)
+                load_spread()
             if n + 1 < MODELS:
                 load_x(n + 1, 0, ROWS)
 
@@ -118,29 +128,26 @@ def tile_model_pa_t_kernel(tc, x, emb_W, emb_b, enc_W1, enc_b1, out):
         nc.vector.tensor_copy(out=emb_b_sb[:], in_=emb_b_bf[:])
         emb_b_rows = const.tile([P, PACK, P], F32)
 
-        def spread_first_biases():
-            rows_ps = psum_o.tile([P, PACK, P], F32, name="o_ps")
-            for t in range(PACK):
-                nc.tensor.matmul(
-                    rows_ps[:, t, :],
-                    lhsT=emb_b_bf[:, t : t + 1].to_broadcast([P, P]),
-                    rhs=identity[:],
-                    start=(t == 0),
-                    stop=(t == PACK - 1),
-                )
-            nc.vector.tensor_copy(out=emb_b_rows[:], in_=rows_ps[:])
+        def spread_b1_first():
             b1_ps = psum_o.tile([P, FEATURES], F32, name="o_ps")
-            nc.tensor.matmul(
-                b1_ps[:],
-                lhsT=identity[:, 0:1].to_broadcast([P, P]),
-                rhs=b1_first[:],
-                start=True,
-                stop=True,
+            nc.tensor.matmul(b1_ps[:], lhsT=first_row[:], rhs=b1_row[:], start=True, stop=True)
+            b1_banks.append(b1_ps)
+
+        def copy_b1_first():
+            nc.scalar.copy(out=b1_sb[:, 0, :], in_=b1_banks[0][:])
+
+        def make_emb_b_rows():
+            nc.gpsimd.tensor_scalar(
+                out=emb_b_rows[:],
+                in0=emb_b_all[:].rearrange("i (p t) -> i t p", t=PACK),
+                scalar1=1.0,
+                scalar2=0.0,
+                op0=MULT,
+                op1=ADD,
             )
-            nc.vector.tensor_copy(out=b1_sb[:, 0, :], in_=b1_ps[:])
 
         def transpose_x(g):
-            n, h = divmod(g, ROWS // GROUP_ROWS)
+            n, h = divmod(g, HALVES)
             xT_ps = psum_x.tile([P, GROUP_COLS], BF16)
             for m in range(GROUP_ROWS):
                 nc.tensor.transpose(
@@ -159,7 +166,7 @@ def tile_model_pa_t_kernel(tc, x, emb_W, emb_b, enc_W1, enc_b1, out):
             n, h = divmod(part, W_PARTS)
             w_grouped = work.tile([P, W_PART_COLS, PACK], BF16, align_bytes=64)
             w_part = w_tiles[n][:, :, h * W_PART_COLS : (h + 1) * W_PART_COLS]
-            if n < 2:
+            if n < VECTOR_MODELS:
                 nc.vector.tensor_copy(
                     out=w_grouped[:].rearrange("p (c i) t -> p c t i", i=4),
                     in_=w_part.rearrange("p t (c i) -> p c t i", i=4),
@@ -192,8 +199,18 @@ def tile_model_pa_t_kernel(tc, x, emb_W, emb_b, enc_W1, enc_b1, out):
         def lay_bias(g, m):
             e_ps = psum_e.tile([P, PACK, P], F32)
             e_banks[(g, m)] = e_ps
-            if m >= vector_blocks_of(g):
-                for t in range(PACK):
+            if m < vector_blocks_of(g):
+                return
+            for t in range(PACK):
+                if g < PLAIN_GROUPS:
+                    nc.tensor.matmul(
+                        e_ps[:, t, :],
+                        lhsT=emb_b_row[:, t:FEATURES:PACK],
+                        rhs=first_row[:],
+                        start=(t == 0),
+                        stop=False,
+                    )
+                else:
                     nc.tensor.matmul(
                         e_ps[:, t, :],
                         lhsT=emb_b_rows[:, t, :],
@@ -214,15 +231,9 @@ def tile_model_pa_t_kernel(tc, x, emb_W, emb_b, enc_W1, enc_b1, out):
                 )
 
         def embed_blocks(g, blocks):
-            if LONG_RUNS:
-                for m in blocks:
-                    lay_bias(g, m)
-                for m in blocks:
-                    multiply_block(g, m)
-            else:
-                for m in blocks:
-                    lay_bias(g, m)
-                    multiply_block(g, m)
+            for m in blocks:
+                lay_bias(g, m)
+                multiply_block(g, m)
 
         def empty_block(g, m):
             if m == GROUP_ROWS - 1:
@@ -251,7 +262,7 @@ def tile_model_pa_t_kernel(tc, x, emb_W, emb_b, enc_W1, enc_b1, out):
             e_codes[g] = (codes, scales)
 
         def encode(g):
-            n = g // (ROWS // GROUP_ROWS)
+            n = g // HALVES
             codes, scales = e_codes[g]
             wc, ws = w_codes[n]
             banks = []
@@ -267,65 +278,86 @@ def tile_model_pa_t_kernel(tc, x, emb_W, emb_b, enc_W1, enc_b1, out):
                     start=True,
                     stop=True,
                 )
-            o_tiles[g] = banks
+            o_banks[g] = banks
 
-        def add_bias(g):
-            n = g // (ROWS // GROUP_ROWS)
-            o_sb = results.tile([P, GROUP_ROWS, FEATURES], F32)
-            for m in range(GROUP_ROWS):
+        def add_bias(g, rows, cols=slice(0, FEATURES)):
+            n = g // HALVES
+            if g not in o_tiles:
+                o_sb = results.tile([P, GROUP_ROWS, FEATURES], F32)
+                o_tiles[g] = o_sb
+            for m in rows:
                 nc.vector.tensor_tensor(
-                    out=o_sb[:, m, :], in0=o_tiles[g][m][:], in1=b1_sb[:, n, :], op=ADD
+                    out=o_tiles[g][:, m, cols], in0=o_banks[g][m][:, cols], in1=b1_sb[:, n, cols], op=ADD
                 )
-            o_tiles[g] = o_sb
 
-        def finish(g):
-            n, h = divmod(g, ROWS // GROUP_ROWS)
-            o_sb = o_tiles[g]
-            rows = 1 if FINE_END and g == GROUPS - 1 else STORE_ROWS
-            for m in range(0, GROUP_ROWS, rows):
-                part = o_sb[:, m : m + rows, :]
-                nc.scalar.activation(out=part, in_=part, func=ACT.Gelu_apprx_tanh)
-                r = h * GROUP_ROWS + m
-                nc.sync.dma_start(out=out_by_model[n][:, r : r + rows, :], in_=part)
+        def gelu_store(g, first, rows, cols=slice(0, FEATURES)):
+            n, h = divmod(g, HALVES)
+            part = o_tiles[g][:, first : first + rows, cols]
+            nc.scalar.activation(out=part, in_=part, func=ACT.Gelu_apprx_tanh)
+            r = h * GROUP_ROWS + first
+            nc.sync.dma_start(out=out_by_model[n][:, r : r + rows, cols], in_=part)
 
         ahead = [3, 2, 1]
         last = GROUPS - 1
+        late_rows = 1
         ctx.enter_context(tc.manual_schedule())
         transpose_x(0)
         copy_xT(0)
-        spread_first_biases()
+
+        embed_blocks(0, ahead)
         transpose_x(1)
-        copy_xT(1)
+        spread_b1_first()
         regroup_w(0)
         regroup_w(1)
         quantise_w(0)
         quantise_w(1)
-        embed_blocks(0, ahead)
+        if VECTOR_MODELS < 2:
+            regroup_w(2)
+            regroup_w(3)
+        make_emb_b_rows()
         for step in range(GROUPS + 2):
             embedding, encoding, finishing = step, step - 1, step - 2
-            if 0 <= encoding < GROUPS and not (EARLY_LAST and encoding == last):
+            if 0 <= encoding < last:
                 quantise_e(encoding)
-            if embedding == 1:
+            if VECTOR_MODELS == 2 and embedding == 1:
                 regroup_w(2)
                 regroup_w(3)
-            if 1 <= embedding < GROUPS - 1:
+            if 1 <= embedding < last:
                 quantise_w(embedding + 1)
                 if embedding + 3 < GROUPS:
                     regroup_w(embedding + 3)
+            if late_rows and 0 <= finishing < last:
+                add_bias(finishing, range(GROUP_ROWS - late_rows, GROUP_ROWS))
             if embedding < GROUPS:
                 for m in ahead:
                     empty_block(embedding, m)
+                    if embedding == 0 and m == 3:
+                        copy_xT(1)
+                        copy_b1_first()
                 embed_blocks(embedding, [0])
             if 0 <= encoding < GROUPS:
                 encode(encoding)
             if embedding < GROUPS:
                 empty_block(embedding, 0)
-            if EARLY_LAST and embedding == last:
+            if embedding == last:
                 quantise_e(embedding)
-            if 0 <= encoding < GROUPS:
-                add_bias(encoding)
-            if 0 <= finishing < GROUPS:
-                finish(finishing)
+            if 0 <= encoding < last:
+                add_bias(encoding, range(GROUP_ROWS - late_rows))
+            if 0 <= finishing < last:
+                rows = 1 if finishing >= GROUPS - 3 else STORE_ROWS
+                for m in range(0, GROUP_ROWS, rows):
+                    gelu_store(finishing, m, rows)
+            if encoding == last:
+                for m in range(GROUP_ROWS - 1):
+                    add_bias(last, [m])
+                half = FEATURES // 2
+                for cols in (slice(0, half), slice(half, FEATURES)):
+                    add_bias(last, [GROUP_ROWS - 1], cols)
+            if finishing == last:
+                for m in range(GROUP_ROWS - 1):
+                    gelu_store(last, m, 1)
+                for cols in (slice(0, half), slice(half, FEATURES)):
+                    gelu_store(last, GROUP_ROWS - 1, 1, cols)
             if embedding + 2 < GROUPS:
                 transpose_x(embedding + 2)
                 copy_xT(embedding + 2)

@@ -26,7 +26,7 @@ STORE_ROWS = 4
 W_PARTS = 2
 W_PART_COLS = FEATURES // W_PARTS
 PLAIN_GROUPS = 4
-VECTOR_MODELS = 1
+VECTOR_MODELS = 2
 
 FLOPS = 2 * MODELS * ROWS * P * FEATURES * (SAMPLES + FEATURES)
 
@@ -96,7 +96,6 @@ def tile_model_pa_t_kernel(tc, x, emb_W, emb_b, enc_W1, enc_b1, out):
         nc.sync.dma_start(out=b1_row[0:1, :], in_=enc_b1[0:1, :])
         load_x(1, 0, ROWS)
         b1_sb = const.tile([P, MODELS, FEATURES], BF16)
-        emb_b_all = const.tile([P, FEATURES], BF16)
 
         def load_spread():
             nc.sync.dma_start(
@@ -106,8 +105,6 @@ def tile_model_pa_t_kernel(tc, x, emb_W, emb_b, enc_W1, enc_b1, out):
 
         for n in range(1, MODELS):
             load_w(n)
-            if n == 1:
-                nc.sync.dma_start(out=emb_b_all[:], in_=emb_b.partition_broadcast(P))
             if n == 2:
                 load_spread()
             if n + 1 < MODELS:
@@ -136,15 +133,19 @@ def tile_model_pa_t_kernel(tc, x, emb_W, emb_b, enc_W1, enc_b1, out):
         def copy_b1_first():
             nc.scalar.copy(out=b1_sb[:, 0, :], in_=b1_banks[0][:])
 
-        def make_emb_b_rows():
-            nc.gpsimd.tensor_scalar(
-                out=emb_b_rows[:],
-                in0=emb_b_all[:].rearrange("i (p t) -> i t p", t=PACK),
-                scalar1=1.0,
-                scalar2=0.0,
-                op0=MULT,
-                op1=ADD,
+        def spread_emb_b():
+            rows_ps = psum_o.tile([P, PACK, P], F32, name="o_ps")
+            nc.tensor.matmul(
+                rows_ps[:],
+                lhsT=first_row[:],
+                rhs=emb_b_row[:].rearrange("k (p t) -> k t p", t=PACK),
+                start=True,
+                stop=True,
             )
+            b1_banks.append(rows_ps)
+
+        def copy_emb_b_rows():
+            nc.scalar.copy(out=emb_b_rows[:], in_=b1_banks[1][:])
 
         def transpose_x(g):
             n, h = divmod(g, HALVES)
@@ -307,6 +308,7 @@ def tile_model_pa_t_kernel(tc, x, emb_W, emb_b, enc_W1, enc_b1, out):
         embed_blocks(0, ahead)
         transpose_x(1)
         spread_b1_first()
+        spread_emb_b()
         regroup_w(0)
         regroup_w(1)
         quantise_w(0)
@@ -314,7 +316,6 @@ def tile_model_pa_t_kernel(tc, x, emb_W, emb_b, enc_W1, enc_b1, out):
         if VECTOR_MODELS < 2:
             regroup_w(2)
             regroup_w(3)
-        make_emb_b_rows()
         for step in range(GROUPS + 2):
             embedding, encoding, finishing = step, step - 1, step - 2
             if 0 <= encoding < last:
@@ -334,6 +335,8 @@ def tile_model_pa_t_kernel(tc, x, emb_W, emb_b, enc_W1, enc_b1, out):
                     if embedding == 0 and m == 3:
                         copy_xT(1)
                         copy_b1_first()
+                if embedding == 0:
+                    copy_emb_b_rows()
                 embed_blocks(embedding, [0])
             if 0 <= encoding < GROUPS:
                 encode(encoding)

@@ -80,16 +80,17 @@ def tile_model_pa_t_kernel(tc, x, emb_W, emb_b, enc_W1, enc_b1, out):
 
         emb_w_sb = const.tile([P, FEATURES], BF16)
         emb_b_bf = const.tile([P, PACK], BF16)
-        emb_b_row = const.tile([P, FEATURES], BF16)
+        emb_b_row = const.tile([1, FEATURES], BF16)
+        emb_b_turned = const.tile([P, PACK, P], BF16)
         b1_row = const.tile([P, FEATURES], BF16)
         first_row = const.tile([P, P], BF16)
-        nc.vector.memset(emb_b_row[:], 0.0)
+        nc.vector.memset(emb_b_turned[:], 0.0)
         nc.vector.memset(first_row[:], 0.0)
         nc.vector.memset(first_row[0:1, :], 1.0)
         nc.vector.memset(b1_row[:], 0.0)
         load_x(0, 0, GROUP_ROWS)
         nc.sync.dma_start(out=emb_w_sb[:], in_=emb_W)
-        nc.sync.dma_start(out=emb_b_row[0:1, :], in_=emb_b.rearrange("(o f) -> o f", o=1))
+        nc.sync.dma_start(out=emb_b_row[:], in_=emb_b.rearrange("(o f) -> o f", o=1))
         load_w(0)
         nc.sync.dma_start(out=emb_b_bf[:], in_=emb_b.rearrange("(p t) -> p t", t=PACK))
         load_x(0, GROUP_ROWS, ROWS)
@@ -121,6 +122,9 @@ def tile_model_pa_t_kernel(tc, x, emb_W, emb_b, enc_W1, enc_b1, out):
         nc.vector.tensor_copy(
             out=emb_w_t[:], in_=emb_w_sb[:].rearrange("s (p t) -> s t p", t=PACK)
         )
+        nc.vector.tensor_copy(
+            out=emb_b_turned[0:1, :, :], in_=emb_b_row[:].rearrange("o (p t) -> o t p", t=PACK)
+        )
         emb_b_sb = const.tile([P, PACK], F32)
         nc.vector.tensor_copy(out=emb_b_sb[:], in_=emb_b_bf[:])
         emb_b_rows = const.tile([P, PACK, P], F32)
@@ -138,7 +142,7 @@ def tile_model_pa_t_kernel(tc, x, emb_W, emb_b, enc_W1, enc_b1, out):
             nc.tensor.matmul(
                 rows_ps[:],
                 lhsT=first_row[:],
-                rhs=emb_b_row[:].rearrange("k (p t) -> k t p", t=PACK),
+                rhs=emb_b_turned[:],
                 start=True,
                 stop=True,
             )
@@ -206,7 +210,7 @@ def tile_model_pa_t_kernel(tc, x, emb_W, emb_b, enc_W1, enc_b1, out):
                 if g < PLAIN_GROUPS:
                     nc.tensor.matmul(
                         e_ps[:, t, :],
-                        lhsT=emb_b_row[:, t:FEATURES:PACK],
+                        lhsT=emb_b_turned[:, t, :],
                         rhs=first_row[:],
                         start=(t == 0),
                         stop=False,

@@ -22,7 +22,7 @@ GROUP_ROWS = 4
 HALVES = ROWS // GROUP_ROWS
 GROUPS = MODELS * HALVES
 GROUP_COLS = GROUP_ROWS * P
-STORE_ROWS = 4
+STORE_ROWS = 2
 W_PARTS = 2
 W_PART_COLS = FEATURES // W_PARTS
 PLAIN_GROUPS = 4
@@ -61,6 +61,9 @@ def tile_model_pa_t_kernel(tc, x, emb_W, emb_b, enc_W1, enc_b1, out):
         o_banks = {}
         o_tiles = {}
         b1_banks = []
+
+        def on_vector(g, m):
+            return m == 1 or (m == 0 and g % 3 == 0)
 
         def vector_blocks_of(g):
             return 1 if g < 3 else 2 if g % 3 == 0 else 1
@@ -204,7 +207,7 @@ def tile_model_pa_t_kernel(tc, x, emb_W, emb_b, enc_W1, enc_b1, out):
         def lay_bias(g, m):
             e_ps = psum_e.tile([P, PACK, P], F32)
             e_banks[(g, m)] = e_ps
-            if m < vector_blocks_of(g):
+            if on_vector(g, m):
                 return
             for t in range(PACK):
                 if g < PLAIN_GROUPS:
@@ -231,7 +234,7 @@ def tile_model_pa_t_kernel(tc, x, emb_W, emb_b, enc_W1, enc_b1, out):
                     e_banks[(g, m)][:, t, :],
                     lhsT=emb_w_t[:, t, :],
                     rhs=xT_tiles[g][:, m * P : (m + 1) * P],
-                    start=(m < vector_blocks_of(g) and t == 0),
+                    start=(on_vector(g, m) and t == 0),
                     stop=(t == PACK - 1),
                 )
 
@@ -246,7 +249,7 @@ def tile_model_pa_t_kernel(tc, x, emb_W, emb_b, enc_W1, enc_b1, out):
                 grouped_tiles[g] = grouped
             dst = grouped_tiles[g][:, m * P : (m + 1) * P, :]
             src = e_banks[(g, m)][:].rearrange("p t c -> p c t")
-            if m < vector_blocks_of(g):
+            if on_vector(g, m):
                 nc.vector.tensor_tensor(
                     out=dst,
                     in0=src,
@@ -308,7 +311,6 @@ def tile_model_pa_t_kernel(tc, x, emb_W, emb_b, enc_W1, enc_b1, out):
         ctx.enter_context(tc.manual_schedule())
         transpose_x(0)
         copy_xT(0)
-
         embed_blocks(0, ahead)
         transpose_x(1)
         spread_b1_first()
@@ -339,20 +341,26 @@ def tile_model_pa_t_kernel(tc, x, emb_W, emb_b, enc_W1, enc_b1, out):
                     if embedding == 0 and m == 3:
                         copy_xT(1)
                         copy_b1_first()
-                if embedding == 0:
-                    copy_emb_b_rows()
                 embed_blocks(embedding, [0])
             if 0 <= encoding < GROUPS:
                 encode(encoding)
+            parts = []
+            if 0 <= finishing < last:
+                rows = 1 if finishing >= GROUPS - 2 else STORE_ROWS
+                parts = list(range(0, GROUP_ROWS, rows))
+            cut = len(parts) * 2 // 4
+            for m in parts[:cut]:
+                gelu_store(finishing, m, rows)
             if embedding < GROUPS:
                 empty_block(embedding, 0)
+            if embedding == 0:
+                copy_emb_b_rows()
             if embedding == last:
                 quantise_e(embedding)
             if 0 <= encoding < last:
                 add_bias(encoding, range(GROUP_ROWS - late_rows))
             if 0 <= finishing < last:
-                rows = 1 if finishing >= GROUPS - 3 else STORE_ROWS
-                for m in range(0, GROUP_ROWS, rows):
+                for m in parts[cut:]:
                     gelu_store(finishing, m, rows)
             if encoding == last:
                 for m in range(GROUP_ROWS - 1):

@@ -45,7 +45,7 @@ def tile_model_pa_t_kernel(tc, x, emb_W, emb_b, enc_W1, enc_b1, out):
         inputs = ctx.enter_context(tc.tile_pool(name="inputs", bufs=MODELS))
         work = ctx.enter_context(tc.tile_pool(name="work", bufs=2))
         turned = ctx.enter_context(tc.tile_pool(name="turned", bufs=4))
-        results = ctx.enter_context(tc.tile_pool(name="results", bufs=4))
+        results = ctx.enter_context(tc.tile_pool(name="results", bufs=8))
         psum_x = ctx.enter_context(tc.psum_pool(name="psum_x", bufs=1))
         psum_e = ctx.enter_context(tc.psum_pool(name="psum_e", bufs=3))
         psum_o = ctx.enter_context(tc.psum_pool(name="psum_o", bufs=4))

@@ -33,9 +33,7 @@ FLOPS = 2 * MODELS * ROWS * P * FEATURES * (SAMPLES + FEATURES)
 
 def tile_model_pa_t_kernel(tc, x, emb_W, emb_b, enc_W1, enc_b1, out):
     nc = tc.nc
-    x_by_model = x.rearrange("b c t -> (b c t)").rearrange(
-        "(p r n s) -> n p r s", r=ROWS, n=MODELS, s=SAMPLES
-    )
+    x_by_row = x.rearrange("b c t -> (b c t)").rearrange("(p r k) -> p r k", r=ROWS, k=MODELS * SAMPLES)
     out_by_model = out.rearrange("n b c l f -> n (b c l) f").rearrange(
         "n (p r) f -> n p r f", r=ROWS
     )
@@ -68,11 +66,17 @@ def tile_model_pa_t_kernel(tc, x, emb_W, emb_b, enc_W1, enc_b1, out):
         def vector_blocks_of(g):
             return 1 if g < 3 else 2 if g % 3 == 0 else 1
 
-        def load_x(n, first, last):
+        def load_x(first_model, end_model, first, last):
             if first == 0:
-                x_sb = inputs.tile([P, ROWS, SAMPLES], BF16, name="x_sb")
-                x_tiles[n] = x_sb
-            nc.sync.dma_start(out=x_tiles[n][:, first:last, :], in_=x_by_model[n][:, first:last, :])
+                x_sb = const.tile(
+                    [P, ROWS, (end_model - first_model) * SAMPLES], BF16, name="x_sb%d" % first_model
+                )
+                for n in range(first_model, end_model):
+                    x_tiles[n] = (x_sb, (n - first_model) * SAMPLES)
+            nc.sync.dma_start(
+                out=x_tiles[first_model][0][:, first:last, :],
+                in_=x_by_row[:, first:last, first_model * SAMPLES : end_model * SAMPLES],
+            )
 
         def load_w(n):
             w_sb = inputs.tile([P, PACK, FEATURES], BF16)
@@ -91,14 +95,14 @@ def tile_model_pa_t_kernel(tc, x, emb_W, emb_b, enc_W1, enc_b1, out):
         nc.vector.memset(first_row[:], 0.0)
         nc.vector.memset(first_row[0:1, :], 1.0)
         nc.vector.memset(b1_row[:], 0.0)
-        load_x(0, 0, GROUP_ROWS)
+        load_x(0, 1, 0, GROUP_ROWS)
         nc.sync.dma_start(out=emb_w_sb[:], in_=emb_W)
         nc.sync.dma_start(out=emb_b_row[:], in_=emb_b.rearrange("(o f) -> o f", o=1))
         load_w(0)
         nc.sync.dma_start(out=emb_b_bf[:], in_=emb_b.rearrange("(p t) -> p t", t=PACK))
-        load_x(0, GROUP_ROWS, ROWS)
+        load_x(0, 1, GROUP_ROWS, ROWS)
         nc.sync.dma_start(out=b1_row[0:1, :], in_=enc_b1[0:1, :])
-        load_x(1, 0, ROWS)
+        load_x(1, 2, 0, ROWS)
         b1_sb = const.tile([P, MODELS, FEATURES], BF16)
 
         def load_spread():
@@ -107,12 +111,10 @@ def tile_model_pa_t_kernel(tc, x, emb_W, emb_b, enc_W1, enc_b1, out):
                 in_=enc_b1[1:MODELS, :].rearrange("n f -> (n f)").partition_broadcast(P),
             )
 
-        for n in range(1, MODELS):
-            load_w(n)
-            if n == 2:
-                load_spread()
-            if n + 1 < MODELS:
-                load_x(n + 1, 0, ROWS)
+        load_w(1)
+        load_x(2, 4, 0, ROWS)
+        load_w(2)
+        load_spread()
 
         identity = const.tile([P, P], BF16)
         masks.make_identity(nc, identity[:])
@@ -156,11 +158,12 @@ def tile_model_pa_t_kernel(tc, x, emb_W, emb_b, enc_W1, enc_b1, out):
 
         def transpose_x(g):
             n, h = divmod(g, HALVES)
+            x_sb, offset = x_tiles[n]
             xT_ps = psum_x.tile([P, GROUP_COLS], BF16)
             for m in range(GROUP_ROWS):
                 nc.tensor.transpose(
                     xT_ps[:, m * P : (m + 1) * P],
-                    x_tiles[n][:, h * GROUP_ROWS + m, :],
+                    x_sb[:, h * GROUP_ROWS + m, offset : offset + SAMPLES],
                     identity[:],
                 )
             xT_tiles[g] = xT_ps
@@ -324,6 +327,12 @@ def tile_model_pa_t_kernel(tc, x, emb_W, emb_b, enc_W1, enc_b1, out):
             regroup_w(3)
         for step in range(GROUPS + 2):
             embedding, encoding, finishing = step, step - 1, step - 2
+            if step == 0:
+                load_w(3)
+            if step == 1:
+                load_x(4, MODELS, 0, ROWS)
+            if step in (2, 4, 6, 8):
+                load_w(3 + step // 2)
             if 0 <= encoding < last:
                 quantise_e(encoding)
             if VECTOR_MODELS == 2 and embedding == 1:

from contextlib import ExitStack

import concourse.masks as masks
import concourse.mybir as mybir

BF16 = mybir.dt.bfloat16
F32 = mybir.dt.float32
U32 = mybir.dt.uint32
U8 = mybir.dt.uint8
FP8X4 = mybir.dt.float8_e4m3fn_x4
ACT = mybir.ActivationFunctionType
ADD = mybir.AluOpType.add
MULT = mybir.AluOpType.mult

P = 128
PACK = 4
MODELS = 8
SAMPLES = 128
FEATURES = 512
ROWS = 8
GROUP_ROWS = 4
HALVES = ROWS // GROUP_ROWS
GROUPS = MODELS * HALVES
GROUP_COLS = GROUP_ROWS * P
STORE_ROWS = 2
W_PARTS = 2
W_PART_COLS = FEATURES // W_PARTS
PLAIN_GROUPS = 4
VECTOR_MODELS = 2

FLOPS = 2 * MODELS * ROWS * P * FEATURES * (SAMPLES + FEATURES)


def tile_model_pa_t_kernel(tc, x, emb_W, emb_b, enc_W1, enc_b1, out):
    nc = tc.nc
    x_by_row = x.rearrange("b c t -> (b c t)").rearrange("(p r k) -> p r k", r=ROWS, k=MODELS * SAMPLES)
    out_by_model = out.rearrange("n b c l f -> n (b c l) f").rearrange(
        "n (p r) f -> n p r f", r=ROWS
    )

    with ExitStack() as ctx:
        const = ctx.enter_context(tc.tile_pool(name="const", bufs=1))
        inputs = ctx.enter_context(tc.tile_pool(name="inputs", bufs=MODELS))
        work = ctx.enter_context(tc.tile_pool(name="work", bufs=2))
        turned = ctx.enter_context(tc.tile_pool(name="turned", bufs=4))
        results = ctx.enter_context(tc.tile_pool(name="results", bufs=8))
        psum_x = ctx.enter_context(tc.psum_pool(name="psum_x", bufs=1))
        psum_e = ctx.enter_context(tc.psum_pool(name="psum_e", bufs=3))
        psum_o = ctx.enter_context(tc.psum_pool(name="psum_o", bufs=4))

        x_tiles = {}
        w_tiles = {}
        xT_tiles = {}
        w_grouped_tiles = {}
        w_codes = {}
        grouped_tiles = {}
        e_banks = {}
        e_codes = {}
        o_banks = {}
        o_tiles = {}
        b1_banks = []

        def on_vector(g, m):
            return m == 1 or (m == 0 and g % 3 == 0)

        def vector_blocks_of(g):
            return 1 if g < 3 else 2 if g % 3 == 0 else 1

        def load_x(first_model, end_model, first, last):
            if first == 0:
                x_sb = const.tile(
                    [P, ROWS, (end_model - first_model) * SAMPLES], BF16, name="x_sb%d" % first_model
                )
                for n in range(first_model, end_model):
                    x_tiles[n] = (x_sb, (n - first_model) * SAMPLES)
            nc.sync.dma_start(
                out=x_tiles[first_model][0][:, first:last, :],
                in_=x_by_row[:, first:last, first_model * SAMPLES : end_model * SAMPLES],
            )

        def load_w(n):
            w_sb = inputs.tile([P, PACK, FEATURES], BF16)
            nc.sync.dma_start(
                out=w_sb[:], in_=enc_W1[n].rearrange("(p t) f -> p t f", t=PACK)
            )
            w_tiles[n] = w_sb

        emb_w_sb = const.tile([P, FEATURES], BF16)
        emb_b_bf = const.tile([P, PACK], BF16)
        emb_b_row = const.tile([1, FEATURES], BF16)
        emb_b_turned = const.tile([P, PACK, P], BF16)
        b1_row = const.tile([P, FEATURES], BF16)
        first_row = const.tile([P, P], BF16)
        nc.vector.memset(emb_b_turned[:], 0.0)
        nc.vector.memset(first_row[:], 0.0)
        nc.vector.memset(first_row[0:1, :], 1.0)
        nc.vector.memset(b1_row[:], 0.0)
        load_x(0, 1, 0, GROUP_ROWS)
        nc.sync.dma_start(out=emb_w_sb[:], in_=emb_W)
        nc.sync.dma_start(out=emb_b_row[:], in_=emb_b.rearrange("(o f) -> o f", o=1))
        load_w(0)
        nc.sync.dma_start(out=emb_b_bf[:], in_=emb_b.rearrange("(p t) -> p t", t=PACK))
        load_x(0, 1, GROUP_ROWS, ROWS)
        nc.sync.dma_start(out=b1_row[0:1, :], in_=enc_b1[0:1, :])
        load_x(1, 2, 0, ROWS)
        b1_sb = const.tile([P, MODELS, FEATURES], BF16)

        def load_spread():
            nc.sync.dma_start(
                out=b1_sb[:, 1:MODELS, :].rearrange("p n f -> p (n f)"),
                in_=enc_b1[1:MODELS, :].rearrange("n f -> (n f)").partition_broadcast(P),
            )

        load_w(1)
        load_x(2, 4, 0, ROWS)
        load_w(2)
        load_spread()

        identity = const.tile([P, P], BF16)
        masks.make_identity(nc, identity[:])
        identity_f32 = const.tile([P, P], F32)
        masks.make_identity(nc, identity_f32[:])
        warm = const.tile([P, 1], F32)
        nc.vector.memset(warm[:], 0.0)
        nc.scalar.activation(out=warm[:], in_=warm[:], func=ACT.Gelu_apprx_tanh)
        emb_w_t = const.tile([P, PACK, P], BF16)
        nc.vector.tensor_copy(
            out=emb_w_t[:], in_=emb_w_sb[:].rearrange("s (p t) -> s t p", t=PACK)
        )
        nc.vector.tensor_copy(
            out=emb_b_turned[0:1, :, :], in_=emb_b_row[:].rearrange("o (p t) -> o t p", t=PACK)
        )
        emb_b_sb = const.tile([P, PACK], F32)
        nc.vector.tensor_copy(out=emb_b_sb[:], in_=emb_b_bf[:])
        emb_b_rows = const.tile([P, PACK, P], F32)

        def spread_b1_first():
            b1_ps = psum_o.tile([P, FEATURES], F32, name="o_ps")
            nc.tensor.matmul(b1_ps[:], lhsT=first_row[:], rhs=b1_row[:], start=True, stop=True)
            b1_banks.append(b1_ps)

        def copy_b1_first():
            nc.scalar.copy(out=b1_sb[:, 0, :], in_=b1_banks[0][:])

        def spread_emb_b():
            rows_ps = psum_o.tile([P, PACK, P], F32, name="o_ps")
            nc.tensor.matmul(
                rows_ps[:],
                lhsT=first_row[:],
                rhs=emb_b_turned[:],
                start=True,
                stop=True,
            )
            b1_banks.append(rows_ps)

        def copy_emb_b_rows():
            nc.scalar.copy(out=emb_b_rows[:], in_=b1_banks[1][:])

        def transpose_x(g):
            n, h = divmod(g, HALVES)
            x_sb, offset = x_tiles[n]
            xT_ps = psum_x.tile([P, GROUP_COLS], BF16)
            for m in range(GROUP_ROWS):
                nc.tensor.transpose(
                    xT_ps[:, m * P : (m + 1) * P],
                    x_sb[:, h * GROUP_ROWS + m, offset : offset + SAMPLES],
                    identity[:],
                )
            xT_tiles[g] = xT_ps

        def copy_xT(g):
            xT = turned.tile([P, GROUP_COLS], BF16)
            nc.scalar.copy(out=xT[:], in_=xT_tiles[g][:])
            xT_tiles[g] = xT

        def regroup_w(part):
            n, h = divmod(part, W_PARTS)
            w_grouped = work.tile([P, W_PART_COLS, PACK], BF16, align_bytes=64)
            w_part = w_tiles[n][:, :, h * W_PART_COLS : (h + 1) * W_PART_COLS]
            if n < VECTOR_MODELS:
                nc.vector.tensor_copy(
                    out=w_grouped[:].rearrange("p (c i) t -> p c t i", i=4),
                    in_=w_part.rearrange("p t (c i) -> p c t i", i=4),
                )
            else:
                nc.gpsimd.tensor_scalar(
                    out=w_grouped[:],
                    in0=w_part.rearrange("p t c -> p c t"),
                    scalar1=1.0,
                    scalar2=0.0,
                    op0=MULT,
                    op1=ADD,
                )
            w_grouped_tiles[part] = w_grouped

        def quantise_w(part):
            n, h = divmod(part, W_PARTS)
            if h == 0:
                w_code_tile = work.tile([P, FEATURES], U32, align_bytes=64, name="w_codes")
                w_scale_tile = work.tile([P, FEATURES], U8, align_bytes=64, name="w_scales")
                w_codes[n] = (w_code_tile, w_scale_tile)
            codes, scales = w_codes[n]
            cols = slice(h * W_PART_COLS, (h + 1) * W_PART_COLS)
            nc.vector.quantize_mx(
                out=codes[:, cols].bitcast(FP8X4),
                scales=scales[:, cols],
                in_=w_grouped_tiles[part][:].rearrange("p c t -> p (c t)"),
            )

        def lay_bias(g, m):
            e_ps = psum_e.tile([P, PACK, P], F32)
            e_banks[(g, m)] = e_ps
            if on_vector(g, m):
                return
            for t in range(PACK):
                if g < PLAIN_GROUPS:
                    nc.tensor.matmul(
                        e_ps[:, t, :],
                        lhsT=emb_b_turned[:, t, :],
                        rhs=first_row[:],
                        start=(t == 0),
                        stop=False,
                    )
                else:
                    nc.tensor.matmul(
                        e_ps[:, t, :],
                        lhsT=emb_b_rows[:, t, :],
                        rhs=identity_f32[:],
                        is_transpose=True,
                        start=(t == 0),
                        stop=False,
                    )

        def multiply_block(g, m):
            for t in range(PACK):
                nc.tensor.matmul(
                    e_banks[(g, m)][:, t, :],
                    lhsT=emb_w_t[:, t, :],
                    rhs=xT_tiles[g][:, m * P : (m + 1) * P],
                    start=(on_vector(g, m) and t == 0),
                    stop=(t == PACK - 1),
                )

        def embed_blocks(g, blocks):
            for m in blocks:
                lay_bias(g, m)
                multiply_block(g, m)

        def empty_block(g, m):
            if m == GROUP_ROWS - 1:
                grouped = work.tile([P, GROUP_COLS, PACK], BF16, align_bytes=64)
                grouped_tiles[g] = grouped
            dst = grouped_tiles[g][:, m * P : (m + 1) * P, :]
            src = e_banks[(g, m)][:].rearrange("p t c -> p c t")
            if on_vector(g, m):
                nc.vector.tensor_tensor(
                    out=dst,
                    in0=src,
                    in1=emb_b_sb[:].unsqueeze(1).to_broadcast([P, P, PACK]),
                    op=ADD,
                )
            else:
                nc.scalar.copy(out=dst, in_=src)

        def quantise_e(g):
            codes = work.tile([P, GROUP_COLS], U32, align_bytes=64, name="e_codes")
            scales = work.tile([P, GROUP_COLS], U8, align_bytes=64, name="e_scales")
            nc.vector.quantize_mx(
                out=codes[:].bitcast(FP8X4),
                scales=scales[:],
                in_=grouped_tiles[g][:].rearrange("p c t -> p (c t)"),
            )
            e_codes[g] = (codes, scales)

        def encode(g):
            n = g // HALVES
            codes, scales = e_codes[g]
            wc, ws = w_codes[n]
            banks = []
            for m in range(GROUP_ROWS):
                o_ps = psum_o.tile([P, FEATURES], F32)
                banks.append(o_ps)
                nc.tensor.matmul_mx(
                    out=o_ps[:],
                    lhsT=codes[:, m * P : (m + 1) * P].bitcast(FP8X4),
                    lhsT_scale=scales[:, m * P : (m + 1) * P],
                    rhs=wc[:].bitcast(FP8X4),
                    rhs_scale=ws[:],
                    start=True,
                    stop=True,
                )
            o_banks[g] = banks

        def add_bias(g, rows, cols=slice(0, FEATURES)):
            n = g // HALVES
            if g not in o_tiles:
                o_sb = results.tile([P, GROUP_ROWS, FEATURES], F32)
                o_tiles[g] = o_sb
            for m in rows:
                nc.vector.tensor_tensor(
                    out=o_tiles[g][:, m, cols], in0=o_banks[g][m][:, cols], in1=b1_sb[:, n, cols], op=ADD
                )

        def gelu_store(g, first, rows, cols=slice(0, FEATURES)):
            n, h = divmod(g, HALVES)
            part = o_tiles[g][:, first : first + rows, cols]
            nc.scalar.activation(out=part, in_=part, func=ACT.Gelu_apprx_tanh)
            r = h * GROUP_ROWS + first
            nc.sync.dma_start(out=out_by_model[n][:, r : r + rows, cols], in_=part)

        ahead = [3, 2, 1]
        last = GROUPS - 1
        late_rows = 1
        ctx.enter_context(tc.manual_schedule())
        transpose_x(0)
        copy_xT(0)
        embed_blocks(0, ahead)
        transpose_x(1)
        spread_b1_first()
        spread_emb_b()
        regroup_w(0)
        regroup_w(1)
        quantise_w(0)
        quantise_w(1)
        if VECTOR_MODELS < 2:
            regroup_w(2)
            regroup_w(3)
        for step in range(GROUPS + 2):
            embedding, encoding, finishing = step, step - 1, step - 2
            if step == 0:
                load_w(3)
            if step == 1:
                load_x(4, MODELS, 0, ROWS)
            if step in (2, 4, 6, 8):
                load_w(3 + step // 2)
            if 0 <= encoding < last:
                quantise_e(encoding)
            if VECTOR_MODELS == 2 and embedding == 1:
                regroup_w(2)
                regroup_w(3)
            if 1 <= embedding < last:
                quantise_w(embedding + 1)
                if embedding + 3 < GROUPS:
                    regroup_w(embedding + 3)
            if late_rows and 0 <= finishing < last:
                add_bias(finishing, range(GROUP_ROWS - late_rows, GROUP_ROWS))
            if embedding < GROUPS:
                for m in ahead:
                    empty_block(embedding, m)
                    if embedding == 0 and m == 3:
                        copy_xT(1)
                        copy_b1_first()
                embed_blocks(embedding, [0])
            if 0 <= encoding < GROUPS:
                encode(encoding)
            parts = []
            if 0 <= finishing < last:
                rows = 1 if finishing >= GROUPS - 2 else STORE_ROWS
                parts = list(range(0, GROUP_ROWS, rows))
            cut = len(parts) * 2 // 4
            for m in parts[:cut]:
                gelu_store(finishing, m, rows)
            if embedding < GROUPS:
                empty_block(embedding, 0)
            if embedding == 0:
                copy_emb_b_rows()
            if embedding == last:
                quantise_e(embedding)
            if 0 <= encoding < last:
                add_bias(encoding, range(GROUP_ROWS - late_rows))
            if 0 <= finishing < last:
                for m in parts[cut:]:
                    gelu_store(finishing, m, rows)
            if encoding == last:
                for m in range(GROUP_ROWS - 1):
                    add_bias(last, [m])
                half = FEATURES // 2
                for cols in (slice(0, half), slice(half, FEATURES)):
                    add_bias(last, [GROUP_ROWS - 1], cols)
            if finishing == last:
                for m in range(GROUP_ROWS - 1):
                    gelu_store(last, m, 1)
                for cols in (slice(0, half), slice(half, FEATURES)):
                    gelu_store(last, GROUP_ROWS - 1, 1, cols)
            if embedding + 2 < GROUPS:
                transpose_x(embedding + 2)
                copy_xT(embedding + 2)
            if embedding + 1 < GROUPS:
                embed_blocks(embedding + 1, ahead)
